import numpy as np
import ml_dtypes


def mxq(x, axis, fmt="e4m3"):
    dtype, down = {"e4m3": (ml_dtypes.float8_e4m3fn, 7), "e5m2": (ml_dtypes.float8_e5m2, 14)}[fmt]
    v = np.moveaxis(np.asarray(x, np.float32).astype(ml_dtypes.bfloat16).astype(np.float64), axis, -1)
    blocks = v.reshape(v.shape[:-1] + (-1, 32))
    amax = np.abs(blocks).max(-1, keepdims=True)
    byte = np.maximum(np.where(amax > 0, np.frexp(amax)[1] - 1 + 127, 0) - down, 1)
    scale = np.exp2(byte - 127.0)
    codes = (blocks / scale).astype(np.float32).astype(dtype).astype(np.float64)
    return np.moveaxis((codes * scale).reshape(v.shape), -1, axis)


WIDE = False


def mx_kscale(k):
    if not WIDE:
        return np.ones(k)
    levels = np.array([10, -10, 5, -5, 0])
    if k % 512:
        return np.exp2(np.random.permutation(np.resize(levels, k // 32))).repeat(32)
    a = np.empty((k // 512, 16))
    for p in range(k // 512):
        a[p, :8] = np.random.permutation(np.resize(levels, 8))
        for g in range(8):
            far = levels[np.abs(levels - a[p, g]) >= 10]
            a[p, g + 8] = far[np.random.randint(len(far))]
    return np.exp2(a.ravel()).repeat(32)


BF16 = ml_dtypes.bfloat16


def bf(x):
    return np.asarray(x, np.float32).astype(BF16)


def f64(x):
    return np.asarray(x).astype(np.float64)


BS, NF, N, J, NOUT = 2, 512, 512, 3, 512
KC = J * NF
EPS = 1e-5


def draw0():
    s = mx_kscale(N)
    c = mx_kscale(NF)
    t = np.tile(c, J)
    nb = N * np.random.choice([0.5, 0.625, 0.75, 0.875], BS)
    wt = np.random.choice([0.25, 0.5, 0.75, 1.0], (BS, 1, N))
    return {"X": bf(np.random.standard_normal((BS, NF, N)) * s[None, None, :] * c[None, :, None]),
            "W": bf(np.random.standard_normal((BS, N, N, J)) / np.sqrt(N) / s[None, None, :, None]),
            "N_batch": bf(nb),
            "mask": bf(wt),
            "cv1_w": bf(np.random.standard_normal((NOUT, KC)) / np.sqrt(KC) / t[None, :]),
            "cv1_b": bf(np.random.standard_normal(NOUT) * 0.5),
            "cv2_w": bf(np.random.standard_normal((NOUT, KC)) / np.sqrt(KC) / t[None, :]),
            "cv2_b": bf(np.random.standard_normal(NOUT) * 0.5),
            "bn_gamma": bf(1.0 + 0.1 * np.random.standard_normal(NOUT + NOUT)),
            "bn_beta": bf(0.3 * np.random.standard_normal(NOUT + NOUT))}


def core(X, W, N_batch, mask, cv1_w, cv1_b, cv2_w, cv2_b, bn_gamma, bn_beta):
    mk = f64(mask)
    Xq = mxq(f64(X), 2, "e4m3")
    Wq = mxq(f64(W), 2, "e4m3")
    g = Wq.transpose(0, 3, 1, 2) @ Xq.transpose(0, 2, 1)[:, None]
    x1 = g.transpose(0, 1, 3, 2).reshape(BS, KC, N)
    x1q = mxq(x1, 1, "e4m3")
    y1 = (mxq(f64(cv1_w), 1, "e4m3") @ x1q) + f64(cv1_b)[None, :, None]
    z1 = np.maximum(y1, 0.0)
    yl1 = np.maximum((mxq(f64(cv2_w), 1, "e4m3") @ x1q) + f64(cv2_b)[None, :, None], 0.0)
    zb = np.concatenate([yl1, z1], axis=1)
    total = f64(N_batch).sum()
    mean = (zb * mk).sum(axis=(0, 2)) / total
    cz = zb - mean[None, :, None]
    var = (mk * cz * cz).sum(axis=(0, 2)) / total
    zbn = cz * (1.0 / np.sqrt(var + EPS))[None, :, None]
    return (f64(bn_gamma)[None, :, None] * zbn + f64(bn_beta)[None, :, None]) * mk


def e4m3fn_bytes(y):
    return np.clip(np.asarray(y, np.float64), -448.0, 448.0).astype(np.float32).astype(ml_dtypes.float8_e4m3fn).view(np.uint8)


def e4m3fn_values(b):
    return np.asarray(b, np.uint8).view(ml_dtypes.float8_e4m3fn).astype(np.float64)


def setup_inputs():
    d = draw0()
    x0 = np.asarray(d['W']).astype(np.float64)
    s = (np.max(np.abs(x0), axis=(0, 1, 3), keepdims=True) / 448.0).astype(np.float32)
    out = {}
    for k, v in d.items():
        if k == 'W':
            out['W_bytes'] = e4m3fn_bytes(x0 / s.astype(np.float64))
            out['W_scale'] = s
        else:
            out[k] = v
    return out


def reference(X, W_bytes, W_scale, N_batch, mask, cv1_w, cv1_b, cv2_w, cv2_b, bn_gamma, bn_beta):
    return core(X, e4m3fn_values(W_bytes) * W_scale.astype(np.float64), N_batch, mask, cv1_w, cv1_b, cv2_w, cv2_b, bn_gamma, bn_beta)

@@ -1,0 +1,522 @@
+from contextlib import ExitStack
+
+import concourse.mybir as mybir
+from concourse.masks import make_identity
+
+BS, NF, N, J, NOUT = 2, 512, 512, 3, 512
+KC = J * NF
+EPS = 1e-5
+P = 128
+T = 4
+MB = N // P
+CB = 2 * NOUT // P
+NU = BS * MB
+
+F32 = mybir.dt.float32
+BF16 = mybir.dt.bfloat16
+U32 = mybir.dt.uint32
+U8 = mybir.dt.uint8
+FP8 = mybir.dt.float8_e4m3fn
+FP8X4 = mybir.dt.float8_e4m3fn_x4
+ALU = mybir.AluOpType
+ACT = mybir.ActivationFunctionType
+
+FLOPS = 2 * BS * J * N * N * NF + 2 * BS * 2 * NOUT * KC * N
+
+CAST_V = (1152, 256, 384, 1024, 768, 1024, 256, 0)
+CV_AT = (2, 1, 2, 1, 0, 2, 2, 1, 1)
+CV_ON_V = (11,)
+ST_AT = ((), (), (), (), (), (2,), (), (), ())
+FINAL = "GGGVGHGGGGVVVVVV"
+FIN_AT = (1, 1, 3, 0, 2, 0, 2, 0, 3, 2, 2)
+VEC_AT = 3
+CAST_G = (384, 512, 768, 256, 768, 512, 384, 384)
+SCB = 2
+SZ_AT = ((), (), (), (), (), (), (), (0, 1), ())
+SZ2 = ((0, 1), (), (), (), (), (), (), (), (), (), (), ())
+SA2 = ((), (), (), (0,), (), (1,), (), (), (), (), (), ())
+GROUPS = (2, 4, 6, 8)
+G_S = 5
+OPS = 2
+DRAIN = 1
+
+
+def tile_layer_simple_pa_kernel(
+    tc, X, W_bytes, W_scale, N_batch, mask, cv1_w, cv1_b, cv2_w, cv2_b, bn_gamma, bn_beta, out
+):
+    nc = tc.nc
+    with ExitStack() as ctx:
+        keep = ctx.enter_context(tc.tile_pool(name="keep", bufs=1))
+        work = ctx.enter_context(tc.tile_pool(name="work", bufs=3))
+        psum = ctx.enter_context(tc.psum_pool(name="psum", bufs=3))
+        ctx.enter_context(tc.manual_schedule())
+
+        ws = keep.tile([P, T], F32)
+        nc.scalar.dma_start(out=ws[:], in_=W_scale[0, 0].rearrange("(p t) o -> p (t o)", t=T))
+
+        wb = [None] * NU
+        xs = [None] * BS
+        cvs = []
+
+        def load_w(i):
+            b, mb = divmod(i, MB)
+            t = keep.tile([P, N * J], U8, name=f"wb{i}")
+            nc.sync.dma_start(
+                out=t[:], in_=W_bytes[b].rearrange("(mb p) n j -> mb p (n j)", p=P)[mb]
+            )
+            wb[i] = t
+
+        def load_x(b):
+            t = keep.tile([P, T, N], BF16, name=f"xs{b}")
+            for h in range(2):
+                nc.sync.dma_start(
+                    out=t[:, 2 * h : 2 * h + 2, :],
+                    in_=X[b].rearrange("(f t) n -> f t n", t=T)[:, 2 * h : 2 * h + 2, :],
+                )
+            xs[b] = t
+
+        def load_cv(cb):
+            src = cv2_w if cb < CB // 2 else cv1_w
+            t = keep.tile([P, KC], BF16, name=f"cvs{cb}")
+            r0 = (cb % (CB // 2)) * P
+            nc.sync.dma_start(out=t[:], in_=src[r0 : r0 + P, :])
+            cvs.append(t)
+
+        ident_b = keep.tile([P, P], BF16)
+        make_identity(nc, ident_b[:])
+        ident_f = keep.tile([P, P], F32)
+        make_identity(nc, ident_f[:])
+        mrow = keep.tile([P, BS * N], BF16)
+        vrow = keep.tile([P, P], BF16)
+        nc.gpsimd.memset(vrow[:], 0.0)
+        nc.gpsimd.memset(mrow[:], 0.0)
+        eps = keep.tile([P, 1], F32)
+        ones = keep.tile([P, P], BF16)
+        nc.gpsimd.memset(ones[:], 1.0)
+
+        load_w(0)
+        load_x(0)
+        load_w(1)
+        load_w(2)
+        load_cv(0)
+        load_w(3)
+        load_cv(1)
+        for b in range(BS):
+            nc.sync.dma_start(out=mrow[0:1, b * N : (b + 1) * N], in_=mask[b])
+        nc.sync.dma_start(out=vrow[0:4, :], in_=cv2_b.rearrange("(r c) -> r c", c=P))
+        nc.sync.dma_start(out=vrow[4:8, :], in_=cv1_b.rearrange("(r c) -> r c", c=P))
+        nc.sync.dma_start(out=vrow[8:16, :], in_=bn_gamma.rearrange("(r c) -> r c", c=P))
+        nc.sync.dma_start(out=vrow[16:24, :], in_=bn_beta.rearrange("(r c) -> r c", c=P))
+        nbt = keep.tile([P, BS], BF16)
+        nc.sync.dma_start(out=nbt[:], in_=N_batch.partition_broadcast(P))
+        load_w(4)
+        load_cv(2)
+        load_x(1)
+        load_w(5)
+        load_cv(3)
+        load_w(6)
+        load_w(7)
+        for cb in range(4, CB):
+            load_cv(cb)
+
+        warm = keep.tile([P, 1], F32)
+        nc.vector.memset(warm[:], 1.0)
+        warm2 = keep.tile([P, 1], F32)
+        nc.scalar.activation(out=warm2[:], in_=warm[:], func=ACT.Sqrt)
+
+        xq = [keep.tile([P, T * P], U32, name=f"xq{b}", align_bytes=64) for b in range(BS)]
+        xsc = [keep.tile([P, T * P], U8, name=f"xsc{b}", align_bytes=64) for b in range(BS)]
+        xg = {}
+
+        def x_turn(b):
+            xg[b] = work.tile([P, T * P * T], BF16, name="xg", align_bytes=64)
+            words = xs[b][:].bitcast(F32).rearrange("p t (q u) -> p t u q", u=2)
+            for h in range(2):
+                ps = psum.tile([P, 2, 2, P], F32, name="y")
+                for i in range(2):
+                    for u in range(2):
+                        nc.tensor.transpose(ps[:, i, u, :], words[:, 2 * h + i, u, :], ident_f[:])
+                nc.scalar.copy(
+                    out=xg[b][:, h * 1024 : (h + 1) * 1024].bitcast(F32).rearrange("p (i f u) -> p i f u", i=2, u=2),
+                    in_=ps[:].rearrange("p i u f -> p i f u"),
+                )
+
+        def x_quant(b):
+            nc.vector.quantize_mx(out=xq[b][:].bitcast(FP8X4), scales=xsc[b][:], in_=xg[b][:])
+
+        cvq = keep.tile([P, CB * J, P], U32, align_bytes=64)
+        cvsc = keep.tile([P, CB * J, P], U8, align_bytes=64)
+        cvg = {}
+        cps = {}
+
+        def cv_turn(h):
+            if h % 2 == 0:
+                cvg[h // 2] = work.tile([P, 4 * P * T], BF16, name="cvg", align_bytes=64)
+            cps[h] = psum.tile([P, 2, 2, P], F32, name="y")
+            for i in range(2):
+                cb, g = divmod(2 * h + i, J)
+                words = cvs[cb][:].bitcast(F32).rearrange("p (g q u) -> p g u q", g=J, u=2)
+                for u in range(2):
+                    nc.tensor.transpose(cps[h][:, i, u, :], words[:, g, u, :], ident_f[:])
+
+        def cv_copy(h):
+            o = (h % 2) * 1024
+            dst = cvg[h // 2][:, o : o + 1024].bitcast(F32).rearrange("p (i f u) -> p i f u", i=2, u=2)
+            src = cps[h][:].rearrange("p i u f -> p i f u")
+            if h in CV_ON_V:
+                nc.vector.tensor_copy(out=dst, in_=src)
+            else:
+                nc.scalar.copy(out=dst, in_=src)
+
+        def cv_quant(h):
+            s4 = 4 * h
+            nc.vector.quantize_mx(
+                out=cvq[:, s4 : s4 + 4, :].rearrange("p g c -> p (g c)").bitcast(FP8X4),
+                scales=cvsc[:, s4 : s4 + 4, :].rearrange("p g c -> p (g c)"),
+                in_=cvg[h][:],
+            )
+
+        x1g = [keep.tile([P, J, N * T], BF16, name=f"x1g{b}", align_bytes=64) for b in range(BS)]
+        x1q = [keep.tile([P, J, N], U32, name=f"x1q{b}", align_bytes=64) for b in range(BS)]
+        x1s = [keep.tile([P, J, N], U8, name=f"x1s{b}", align_bytes=64) for b in range(BS)]
+        ws_b = ws[:].unsqueeze(1).to_broadcast([P, P, T])
+        wf = {}
+        wg = {}
+        wt = {}
+        wq = {}
+        mm = {}
+
+        def widen(i):
+            wf[i] = work.tile([P, N * J], BF16, name="wf", align_bytes=64)
+            v = CAST_V[i]
+            h = CAST_G[i]
+            if v:
+                nc.vector.tensor_copy(out=wf[i][:, 0:v], in_=wb[i][:, 0:v].bitcast(FP8))
+            if h:
+                nc.gpsimd.tensor_copy(out=wf[i][:, v : v + h], in_=wb[i][:, v : v + h].bitcast(FP8))
+            if v + h < N * J:
+                nc.scalar.copy(out=wf[i][:, v + h :], in_=wb[i][:, v + h :].bitcast(FP8))
+
+        def w_turn(i, j):
+            if j == 0:
+                wg[i] = work.tile([P, J, P * T], BF16, name="wg", align_bytes=64)
+            view = wf[i][:].rearrange("p (q t j) -> p t j q", t=T, j=J)
+            wt[i, j] = psum.tile([P, T, P], BF16, name="tw")
+            for t in range(T):
+                nc.tensor.transpose(wt[i, j][:, t, :], view[:, t, j, :], ident_b[:])
+
+        def w_scale(i, j):
+            nc.vector.tensor_tensor(
+                out=wg[i][:, j, :].rearrange("p (m t) -> p m t", t=T),
+                in0=wt[i, j][:].rearrange("p t m -> p m t"),
+                in1=ws_b,
+                op=ALU.mult,
+            )
+
+        def w_quant(i, lo, hi):
+            if lo == 0:
+                wq[i] = (
+                    work.tile([P, J, P], U32, name="wq", align_bytes=64),
+                    work.tile([P, J, P], U8, name="wsc", align_bytes=64),
+                )
+            q, s = wq[i]
+            nc.vector.quantize_mx(
+                out=q[:, lo:hi, :].rearrange("p j m -> p (j m)").bitcast(FP8X4),
+                scales=s[:, lo:hi, :].rearrange("p j m -> p (j m)"),
+                in_=wg[i][:, lo:hi, :].rearrange("p j m -> p (j m)"),
+            )
+
+        def step1(i, j):
+            b, mb = divmod(i, MB)
+            q, s = wq[i]
+            mm[i, j] = psum.tile([P, T, P], F32, name="mm", bufs=2)
+            for t in range(T):
+                nc.tensor.matmul_mx(
+                    out=mm[i, j][:, t, :],
+                    lhsT=xq[b][:, t * P : (t + 1) * P].bitcast(FP8X4),
+                    lhsT_scale=xsc[b][:, t * P : (t + 1) * P],
+                    rhs=q[:, j, :].bitcast(FP8X4),
+                    rhs_scale=s[:, j, :],
+                    start=True,
+                    stop=True,
+                )
+
+        def x1_copy(i, j):
+            b, mb = divmod(i, MB)
+            nc.scalar.copy(
+                out=x1g[b][:, j, mb * P * T : (mb + 1) * P * T].rearrange("p (m t) -> p m t", t=T),
+                in_=mm[i, j][:].rearrange("p t m -> p m t"),
+            )
+
+        def x1_quant(b, h, j):
+            c0 = h * 2 * P
+            nc.vector.quantize_mx(
+                out=x1q[b][:, j, c0 : c0 + 2 * P].bitcast(FP8X4),
+                scales=x1s[b][:, j, c0 : c0 + 2 * P],
+                in_=x1g[b][:, j, c0 * T : (c0 + 2 * P) * T],
+            )
+
+        vec = keep.tile([P, 3 * CB], F32)
+        bias = vec[:, 0:CB]
+        gamma = vec[:, CB : 2 * CB]
+        beta = vec[:, 2 * CB : 3 * CB]
+        mk = keep.tile([P, BS, N], F32)
+        msum = keep.tile([P, BS], F32)
+        nbias = keep.tile([P, CB], F32)
+        tot = keep.tile([P, 1], F32)
+        rt = keep.tile([P, 1], F32)
+        mtot = keep.tile([P, 1], F32)
+        mr1 = keep.tile([P, 1], F32)
+        bm1 = keep.tile([P, CB], F32)
+        c1 = keep.tile([P, 1], F32)
+        c2 = keep.tile([P, CB], F32)
+
+        def vectors():
+            pv = psum.tile([P, P], BF16, name="y")
+            nc.tensor.transpose(pv[:], vrow[:], ident_b[:])
+            nc.vector.tensor_copy(out=vec[:], in_=pv[:, 0 : 3 * CB])
+            for b in range(BS):
+                pm = psum.tile([P, N], F32, name="y")
+                nc.tensor.matmul(pm[:], lhsT=ones[:], rhs=mrow[:, b * N : (b + 1) * N], start=True, stop=True)
+                nc.scalar.activation(out=mk[:, b, :], in_=pm[:], func=ACT.Copy, accum_out=msum[:, b : b + 1])
+            nc.gpsimd.tensor_tensor(out=tot[:], in0=nbt[:, 0:1], in1=nbt[:, 1:2], op=ALU.add)
+            nc.gpsimd.tensor_scalar(out=eps[:], in0=tot[:], scalar1=0.0, scalar2=EPS, op0=ALU.mult, op1=ALU.add)
+            nc.gpsimd.tensor_scalar(out=nbias[:], in0=bias, scalar1=-1.0, scalar2=0.0, op0=ALU.mult, op1=ALU.add)
+            nc.vector.reciprocal(out=rt[:], in_=tot[:])
+            nc.gpsimd.tensor_tensor(out=mtot[:], in0=msum[:, 0:1], in1=msum[:, 1:2], op=ALU.add)
+            nc.gpsimd.tensor_scalar(out=mr1[:], in0=mtot[:], scalar1=rt[:], scalar2=1.0, op0=ALU.mult, op1=ALU.subtract)
+            nc.gpsimd.memset(bm1[:, 0:SCB], 0.0)
+            nc.gpsimd.tensor_scalar(out=bm1[:, SCB:], in0=bias[:, SCB:], scalar1=mr1[:], scalar2=0.0, op0=ALU.mult, op1=ALU.add)
+            nc.gpsimd.tensor_scalar(out=c1[:], in0=tot[:], scalar1=-2.0, scalar2=mtot[:], op0=ALU.mult, op1=ALU.add)
+            nc.gpsimd.tensor_scalar(out=c2[:], in0=bm1[:], scalar1=tot[:], scalar2=2.0, op0=ALU.mult, op1=ALU.mult)
+
+        st = keep.tile([P, 2, BS, CB], F32)
+        u = {}
+        ys = {}
+        sms = {}
+
+        def conv(cb, b, tag):
+            ys[cb, b] = psum.tile([P, N], F32, name=tag, bufs=2 if tag == "mm" else 3)
+            for j in range(J):
+                nc.tensor.matmul_mx(
+                    out=ys[cb, b][:],
+                    lhsT=cvq[:, cb * J + j, :].bitcast(FP8X4),
+                    lhsT_scale=cvsc[:, cb * J + j, :],
+                    rhs=x1q[b][:, j, :].bitcast(FP8X4),
+                    rhs_scale=x1s[b][:, j, :],
+                    start=(j == 0),
+                    stop=(j == J - 1),
+                )
+
+        def stat1(cb, b):
+            ub = work.tile([P, N], F32, name="u", bufs=16)
+            nc.vector.scalar_tensor_tensor(
+                out=ub[:], in0=ys[cb, b][:], scalar=nbias[:, cb : cb + 1], in1=mk[:, b, :],
+                op0=ALU.max, op1=ALU.mult, accum_out=st[:, 0, b, cb : cb + 1],
+            )
+            u[cb, b] = ub
+
+        def stat2(cb, b):
+            junk = work.tile([P, N], F32, name="junk", bufs=2)
+            nc.vector.scalar_tensor_tensor(
+                out=junk[:], in0=ys[cb, b][:], scalar=nbias[:, cb : cb + 1], in1=u[cb, b][:],
+                op0=ALU.max, op1=ALU.mult, accum_out=st[:, 1, b, cb : cb + 1],
+            )
+
+        g = nc.gpsimd
+        v = nc.vector
+        s12 = keep.tile([P, 2, CB], F32)
+        dd = keep.tile([P, CB], F32)
+        qq = keep.tile([P, CB], F32)
+        vv = keep.tile([P, CB], F32)
+        ww = keep.tile([P, CB], F32)
+        sd = keep.tile([P, CB], F32)
+        rs = keep.tile([P, CB], F32)
+        aa = keep.tile([P, CB], F32)
+        ad = keep.tile([P, CB], F32)
+        nb = keep.tile([P, CB], F32)
+
+        def norm_ops(lo, hi):
+            c = slice(lo, hi)
+            return [
+                lambda: v.tensor_tensor(out=s12[:, :, c], in0=st[:, :, 0, c], in1=st[:, :, 1, c], op=ALU.add),
+                lambda: v.scalar_tensor_tensor(out=dd[:, c], in0=s12[:, 0, c], scalar=rt[:], in1=bm1[:, c], op0=ALU.mult, op1=ALU.add),
+                lambda: v.scalar_tensor_tensor(out=qq[:, c], in0=dd[:, c], scalar=c1[:], in1=c2[:, c], op0=ALU.mult, op1=ALU.add),
+                lambda: v.tensor_tensor(out=vv[:, c], in0=dd[:, c], in1=qq[:, c], op=ALU.mult),
+                lambda: (
+                    v.tensor_tensor(out=ww[:, c], in0=vv[:, c], in1=s12[:, 1, c], op=ALU.add),
+                    nc.scalar.activation(out=sd[:, c], in_=ww[:, c], func=ACT.Sqrt, scale=rt[:], bias=eps[:]),
+                ),
+                lambda: v.reciprocal(out=rs[:, c], in_=sd[:, c]),
+                lambda: v.tensor_tensor(out=aa[:, c], in0=rs[:, c], in1=gamma[:, c], op=ALU.mult),
+                lambda: v.tensor_tensor(out=ad[:, c], in0=aa[:, c], in1=dd[:, c], op=ALU.mult),
+                lambda: (v.tensor_tensor(out=nb[:, c], in0=ad[:, c], in1=beta[:, c], op=ALU.subtract), range(lo, hi))[1],
+            ]
+
+        fin = {}
+
+        sz = {}
+
+        def z_pass(cb, b):
+            z = work.tile([P, N], F32, name="z", bufs=2)
+            nc.scalar.activation(out=z[:], in_=ys[cb, b][:], func=ACT.Relu, bias=bias[:, cb : cb + 1])
+            ub = work.tile([P, N], F32, name="u", bufs=16)
+            g.tensor_tensor(out=ub[:], in0=z[:], in1=mk[:, b, :], op=ALU.mult)
+            q = work.tile([P, N], F32, name="q", bufs=2)
+            g.tensor_tensor(out=q[:], in0=z[:], in1=ub[:], op=ALU.mult)
+            u[cb, b] = ub
+            sz[cb, b] = q
+
+        def z_sums(cb, b):
+            for i, t in enumerate((u[cb, b], sz[cb, b])):
+                junk = work.tile([P, N], F32, name="junks", bufs=2)
+                nc.scalar.activation(out=junk[:], in_=t[:], func=ACT.Copy, accum_out=st[:, i, b, cb : cb + 1])
+
+        def finish_s(cb, b):
+            na = aa[:, cb : cb + 1]
+            nbc = nb[:, cb : cb + 1]
+            kind = FINAL[2 * cb + b]
+            bm = work.tile([P, N], F32, name="bm", bufs=4)
+            au = None
+            if kind == "H":
+                g.tensor_scalar(out=bm[:], in0=mk[:, b, :], scalar1=nbc, scalar2=0.0, op0=ALU.mult, op1=ALU.add)
+            else:
+                nc.scalar.activation(out=bm[:], in_=mk[:, b, :], func=ACT.Copy, scale=nbc)
+            if kind != "V":
+                au = work.tile([P, N], F32, name="au", bufs=4)
+                nc.scalar.activation(out=au[:], in_=u[cb, b][:], func=ACT.Copy, scale=na)
+            fin[cb, b] = (bm, au)
+
+        def finish(cb, b):
+            bm, au = fin[cb, b]
+            o = work.tile([P, N], F32, name="o", bufs=8)
+            if au is None:
+                nc.vector.scalar_tensor_tensor(
+                    out=o[:], in0=u[cb, b][:], scalar=aa[:, cb : cb + 1], in1=bm[:], op0=ALU.mult, op1=ALU.subtract
+                )
+            else:
+                g.tensor_tensor(out=o[:], in0=au[:], in1=bm[:], op=ALU.subtract)
+            nc.sync.dma_start(out=out[b, cb * P : (cb + 1) * P, :], in_=o[:])
+
+        cv_done = [0]
+
+        def cv_banks(n):
+            hs = list(range(cv_done[0], cv_done[0] + n))
+            cv_done[0] += n
+            return hs
+
+        def stats(c):
+            stat1(*c)
+            stat2(*c)
+
+        cvh = [[]]
+        szs = [[]]
+        widen(0)
+        for k in range(NU + 1):
+            hs = cv_banks(CV_AT[k])
+            pre = [(cb, 0) for cb in ST_AT[k]]
+            if k + 1 < NU:
+                widen(k + 1)
+            if k < NU:
+                for j in range(J):
+                    w_turn(k, j)
+            if k % MB == 0 and k < NU:
+                x_turn(k // MB)
+            if k == VEC_AT:
+                vectors()
+            for h in hs:
+                cv_turn(h)
+            for j in range(J):
+                if k > 0:
+                    step1(k - 1, j)
+                    x1_copy(k - 1, j)
+            for h in hs:
+                cv_copy(h)
+            if k < NU:
+                w_scale(k, 0)
+                w_scale(k, 1)
+            if k >= 3 and k % 2 == 1:
+                b, h = divmod((k - 3) // 2, 2)
+                for j in range(J):
+                    x1_quant(b, h, j)
+            if k < NU:
+                w_scale(k, 2)
+                w_quant(k, 0, 2)
+            if k % MB == 0 and k < NU:
+                x_quant(k // MB)
+            for h in cvh[0]:
+                if h % 2 == 1:
+                    cv_quant(h // 2)
+            cvh[0] = hs
+            if k < NU:
+                w_quant(k, 2, 3)
+            for c in pre:
+                conv(*c, "y")
+                stats(c)
+            for c in szs[0]:
+                z_sums(*c)
+            szs[0] = [(cb, 0) for cb in SZ_AT[k]]
+            for c in szs[0]:
+                conv(*c, "y")
+                z_pass(*c)
+        for h in cvh[0]:
+            if h % 2 == 1:
+                cv_quant(h // 2)
+        for j in range(J):
+            x1_quant(1, 1, j)
+
+        done = [(cb, 0) for k in range(NU + 1) for cb in ST_AT[k]]
+        todo = [(cb, b) for cb in range(CB) for b in range(BS) if cb >= SCB and (cb, b) not in done]
+        tags = ("y", "tw", "mm")
+        conv_of = {c: tags[i % 3] for i, c in enumerate(todo)}
+        ahead = [0]
+
+        def conv_next(n):
+            for c in todo[ahead[0] : ahead[0] + n]:
+                conv(*c, conv_of[c])
+            ahead[0] += n
+
+        for c in szs[0]:
+            z_sums(*c)
+        wait = []
+        ops = []
+        start = SCB
+        for cb in SZ2[0]:
+            conv(cb, 1, "tw")
+        conv_next(5)
+
+        def norm_some(n):
+            for op in ops[:n]:
+                done_now = op()
+                if isinstance(done_now, range):
+                    wait.extend((cb, b) for cb in done_now for b in range(BS))
+            return ops[n:]
+
+        for i, c in enumerate(todo):
+            for cb in SZ2[i]:
+                z_pass(cb, 1)
+            for cb in SA2[i]:
+                z_sums(cb, 1)
+            if i == G_S and SCB:
+                ops = ops + norm_ops(0, SCB)
+            now = wait[: FIN_AT[i]]
+            wait = wait[FIN_AT[i] :]
+            for f in now:
+                finish_s(*f)
+            for half in (stat1, stat2):
+                half(*c)
+                ops = norm_some(OPS)
+            conv_next(1)
+            for f in now:
+                finish(*f)
+            if c[1] == BS - 1 and c[0] + 1 in GROUPS:
+                ops = ops + norm_ops(start, c[0] + 1)
+                start = c[0] + 1
+        head = wait[:DRAIN]
+        for f in head:
+            finish_s(*f)
+        ops = norm_some(len(ops))
+        for i, f in enumerate(wait):
+            if i >= len(head):
+                finish_s(*f)
+            finish(*f)

@@ -23,22 +23,22 @@ ACT = mybir.ActivationFunctionType
 
 FLOPS = 2 * BS * J * N * N * NF + 2 * BS * 2 * NOUT * KC * N
 
-CAST_V = (1152, 256, 384, 1024, 768, 1024, 256, 0)
-CV_AT = (2, 1, 2, 1, 0, 2, 2, 1, 1)
-CV_ON_V = (11,)
-ST_AT = ((), (), (), (), (), (2,), (), (), ())
-FINAL = "GGGVGHGGGGVVVVVV"
-FIN_AT = (1, 1, 3, 0, 2, 0, 2, 0, 3, 2, 2)
-VEC_AT = 3
-CAST_G = (384, 512, 768, 256, 768, 512, 384, 384)
-SCB = 2
-SZ_AT = ((), (), (), (), (), (), (), (0, 1), ())
-SZ2 = ((0, 1), (), (), (), (), (), (), (), (), (), (), ())
-SA2 = ((), (), (), (0,), (), (1,), (), (), (), (), (), ())
-GROUPS = (2, 4, 6, 8)
+CV_AT = (1, 1, 2, 1, 0, 2, 1, 0, 1, 0, 1, 2, 0)
+CV_ON_V = (10,)
+VEC_AT = 1
+X1_AT = 4
+SCB = 3
+SZ_AT = ((), (), (), (), (), (), (), (0,), (), (1,), (), (2,), ())
+ST_AT = ((), (), (), (), (), (), (), (), (), (), (), (), (3,))
+SZ2 = ((0, 1), (2,), (), (), (), (), (), (), (), ())
+SA2 = ((), (), (), (0,), (1, 2), (), (), (), (), ())
+GROUPS = (3, 6, 8)
 G_S = 5
-OPS = 2
-DRAIN = 1
+OPS = 5
+AHEAD = 5
+DRAIN = 2
+FINAL = "VGGVVVHGVGGVVVVV"
+FIN_AT = (1, 0, 1, 1, 2, 0, 2, 2, 3)
 
 
 def tile_layer_simple_pa_kernel(
@@ -95,8 +95,8 @@ def tile_layer_simple_pa_kernel(
         nc.gpsimd.memset(ones[:], 1.0)
 
         load_w(0)
-        load_x(0)
         load_w(1)
+        load_x(0)
         load_w(2)
         load_cv(0)
         load_w(3)
@@ -179,7 +179,9 @@ def tile_layer_simple_pa_kernel(
         x1g = [keep.tile([P, J, N * T], BF16, name=f"x1g{b}", align_bytes=64) for b in range(BS)]
         x1q = [keep.tile([P, J, N], U32, name=f"x1q{b}", align_bytes=64) for b in range(BS)]
         x1s = [keep.tile([P, J, N], U8, name=f"x1s{b}", align_bytes=64) for b in range(BS)]
-        ws_b = ws[:].unsqueeze(1).to_broadcast([P, P, T])
+        ws_b = ws[:].rearrange("p (u e) -> p u e", u=2).unsqueeze(1).to_broadcast([P, 2 * P, 2, 2])
+        one = keep.tile([P, 1], F32)
+        nc.vector.memset(one[:], 1.0)
         wf = {}
         wg = {}
         wt = {}
@@ -187,65 +189,60 @@ def tile_layer_simple_pa_kernel(
         mm = {}
 
         def widen(i):
-            wf[i] = work.tile([P, N * J], BF16, name="wf", align_bytes=64)
-            v = CAST_V[i]
-            h = CAST_G[i]
-            if v:
-                nc.vector.tensor_copy(out=wf[i][:, 0:v], in_=wb[i][:, 0:v].bitcast(FP8))
-            if h:
-                nc.gpsimd.tensor_copy(out=wf[i][:, v : v + h], in_=wb[i][:, v : v + h].bitcast(FP8))
-            if v + h < N * J:
-                nc.scalar.copy(out=wf[i][:, v + h :], in_=wb[i][:, v + h :].bitcast(FP8))
+            wf[i] = work.tile([P, J, N], BF16, name="wf", bufs=4)
+            nc.vector.tensor_scalar(
+                out=wf[i][:].rearrange("p j n -> p n j"),
+                in0=wb[i][:].rearrange("p (n j) -> p n j", j=J).bitcast(FP8),
+                scalar1=one[:],
+                scalar2=None,
+                op0=ALU.mult,
+            )
 
-        def w_turn(i, j):
-            if j == 0:
-                wg[i] = work.tile([P, J, P * T], BF16, name="wg", align_bytes=64)
-            view = wf[i][:].rearrange("p (q t j) -> p t j q", t=T, j=J)
-            wt[i, j] = psum.tile([P, T, P], BF16, name="tw")
-            for t in range(T):
-                nc.tensor.transpose(wt[i, j][:, t, :], view[:, t, j, :], ident_b[:])
+        def w_turn(r):
+            s, j = divmod(r, J)
+            wt[r] = psum.tile([P, 2, 2 * P], F32, name="tw", bufs=2)
+            for h in range(2):
+                words = wf[2 * s + h][:, j, :].bitcast(F32).rearrange("p (q u) -> p u q", u=2)
+                for e in range(2):
+                    nc.tensor.transpose(wt[r][:, e, h * P : (h + 1) * P], words[:, e, :], ident_f[:])
 
-        def w_scale(i, j):
+        def w_scale(r):
+            wg[r] = work.tile([P, 2 * P * T], BF16, name="wg", align_bytes=64)
             nc.vector.tensor_tensor(
-                out=wg[i][:, j, :].rearrange("p (m t) -> p m t", t=T),
-                in0=wt[i, j][:].rearrange("p t m -> p m t"),
+                out=wg[r][:].rearrange("p (m u e) -> p m u e", u=2, e=2),
+                in0=wt[r][:].rearrange("p u m -> p (u m)").bitcast(BF16).rearrange("p (u m e) -> p m u e", u=2, e=2),
                 in1=ws_b,
                 op=ALU.mult,
             )
 
-        def w_quant(i, lo, hi):
-            if lo == 0:
-                wq[i] = (
-                    work.tile([P, J, P], U32, name="wq", align_bytes=64),
-                    work.tile([P, J, P], U8, name="wsc", align_bytes=64),
-                )
-            q, s = wq[i]
-            nc.vector.quantize_mx(
-                out=q[:, lo:hi, :].rearrange("p j m -> p (j m)").bitcast(FP8X4),
-                scales=s[:, lo:hi, :].rearrange("p j m -> p (j m)"),
-                in_=wg[i][:, lo:hi, :].rearrange("p j m -> p (j m)"),
-            )
+        def w_quant(r):
+            q = work.tile([P, 2 * P], U32, name="wq", align_bytes=64)
+            s = work.tile([P, 2 * P], U8, name="wsc", align_bytes=64)
+            nc.vector.quantize_mx(out=q[:].bitcast(FP8X4), scales=s[:], in_=wg[r][:])
+            wq[r] = (q, s)
 
-        def step1(i, j):
-            b, mb = divmod(i, MB)
-            q, s = wq[i]
-            mm[i, j] = psum.tile([P, T, P], F32, name="mm", bufs=2)
+        def step1(r, h):
+            s, j = divmod(r, J)
+            b = s // 2
+            q, sc = wq[r]
+            mm[r, h] = psum.tile([P, T, P], F32, name="mm", bufs=3)
             for t in range(T):
                 nc.tensor.matmul_mx(
-                    out=mm[i, j][:, t, :],
+                    out=mm[r, h][:, t, :],
                     lhsT=xq[b][:, t * P : (t + 1) * P].bitcast(FP8X4),
                     lhsT_scale=xsc[b][:, t * P : (t + 1) * P],
-                    rhs=q[:, j, :].bitcast(FP8X4),
-                    rhs_scale=s[:, j, :],
+                    rhs=q[:, h * P : (h + 1) * P].bitcast(FP8X4),
+                    rhs_scale=sc[:, h * P : (h + 1) * P],
                     start=True,
                     stop=True,
                 )
 
-        def x1_copy(i, j):
-            b, mb = divmod(i, MB)
+        def x1_copy(r, h):
+            s, j = divmod(r, J)
+            c0 = (2 * (s % 2) + h) * P * T
             nc.scalar.copy(
-                out=x1g[b][:, j, mb * P * T : (mb + 1) * P * T].rearrange("p (m t) -> p m t", t=T),
-                in_=mm[i, j][:].rearrange("p t m -> p m t"),
+                out=x1g[s // 2][:, j, c0 : c0 + P * T].rearrange("p (m t) -> p m t", t=T),
+                in_=mm[r, h][:].rearrange("p t m -> p m t"),
             )
 
         def x1_quant(b, h, j):
@@ -296,7 +293,7 @@ def tile_layer_simple_pa_kernel(
         sms = {}
 
         def conv(cb, b, tag):
-            ys[cb, b] = psum.tile([P, N], F32, name=tag, bufs=2 if tag == "mm" else 3)
+            ys[cb, b] = psum.tile([P, N], F32, name=tag, bufs=2 if tag == "tw" else 3)
             for j in range(J):
                 nc.tensor.matmul_mx(
                     out=ys[cb, b][:],
@@ -409,81 +406,77 @@ def tile_layer_simple_pa_kernel(
             stat1(*c)
             stat2(*c)
 
-        cvh = [[]]
-        szs = [[]]
+        R = BS * J * MB // 2
+        cvh = []
+        szs = []
         widen(0)
-        for k in range(NU + 1):
-            hs = cv_banks(CV_AT[k])
-            pre = [(cb, 0) for cb in ST_AT[k]]
-            if k + 1 < NU:
-                widen(k + 1)
-            if k < NU:
-                for j in range(J):
-                    w_turn(k, j)
-            if k % MB == 0 and k < NU:
-                x_turn(k // MB)
-            if k == VEC_AT:
+        widen(1)
+        w_turn(0)
+        x_turn(0)
+        for r in range(R + 1):
+            hs = cv_banks(CV_AT[r])
+            if r == 1:
+                x_quant(0)
+            if r > 0:
+                w_quant(r - 1)
+                for h in range(2):
+                    step1(r - 1, h)
+                    x1_copy(r - 1, h)
+            if r < R:
+                w_scale(r)
+            if r % J and r + J - r % J < R:
+                widen(2 * (r // J + 1) + r % J - 1)
+            if r + 1 < R:
+                w_turn(r + 1)
+            if r == X1_AT:
+                x_turn(1)
+            if r == X1_AT + 1:
+                x_quant(1)
+            if r == VEC_AT:
                 vectors()
             for h in hs:
                 cv_turn(h)
-            for j in range(J):
-                if k > 0:
-                    step1(k - 1, j)
-                    x1_copy(k - 1, j)
-            for h in hs:
                 cv_copy(h)
-            if k < NU:
-                w_scale(k, 0)
-                w_scale(k, 1)
-            if k >= 3 and k % 2 == 1:
-                b, h = divmod((k - 3) // 2, 2)
-                for j in range(J):
-                    x1_quant(b, h, j)
-            if k < NU:
-                w_scale(k, 2)
-                w_quant(k, 0, 2)
-            if k % MB == 0 and k < NU:
-                x_quant(k // MB)
-            for h in cvh[0]:
+            if r >= 2:
+                s, j = divmod(r - 2, J)
+                x1_quant(s // 2, s % 2, j)
+            for h in cvh:
                 if h % 2 == 1:
                     cv_quant(h // 2)
-            cvh[0] = hs
-            if k < NU:
-                w_quant(k, 2, 3)
-            for c in pre:
-                conv(*c, "y")
-                stats(c)
-            for c in szs[0]:
+            cvh = hs
+            for cb in ST_AT[r]:
+                conv(cb, 0, "y")
+                stats((cb, 0))
+            for c in szs:
                 z_sums(*c)
-            szs[0] = [(cb, 0) for cb in SZ_AT[k]]
-            for c in szs[0]:
+            szs = [(cb, 0) for cb in SZ_AT[r]]
+            for c in szs:
                 conv(*c, "y")
                 z_pass(*c)
-        for h in cvh[0]:
+        for h in cvh:
             if h % 2 == 1:
                 cv_quant(h // 2)
-        for j in range(J):
-            x1_quant(1, 1, j)
+        x1_quant(1, 1, J - 1)
 
-        done = [(cb, 0) for k in range(NU + 1) for cb in ST_AT[k]]
+        done = [(cb, 0) for k in range(R + 1) for cb in ST_AT[k]]
         todo = [(cb, b) for cb in range(CB) for b in range(BS) if cb >= SCB and (cb, b) not in done]
-        tags = ("y", "tw", "mm")
-        conv_of = {c: tags[i % 3] for i, c in enumerate(todo)}
+        seq = []
+        for i, c in enumerate(todo):
+            seq += [(cb, 1) for cb in SZ2[i]] + [c]
+        tags = ("y", "mm", "tw", "y", "mm", "tw", "y", "mm")
         ahead = [0]
 
         def conv_next(n):
-            for c in todo[ahead[0] : ahead[0] + n]:
-                conv(*c, conv_of[c])
+            for i in range(ahead[0], min(ahead[0] + n, len(seq))):
+                conv(*seq[i], tags[i % 8])
             ahead[0] += n
 
-        for c in szs[0]:
+        for c in szs:
             z_sums(*c)
         wait = []
         ops = []
         start = SCB
-        for cb in SZ2[0]:
-            conv(cb, 1, "tw")
-        conv_next(5)
+        conv_next(AHEAD)
 
         def norm_some(n):
             for op in ops[:n]:
@@ -506,7 +499,7 @@ def tile_layer_simple_pa_kernel(
             for half in (stat1, stat2):
                 half(*c)
                 ops = norm_some(OPS)
-            conv_next(1)
+            conv_next(1 + len(SZ2[i]))
             for f in now:
                 finish(*f)
             if c[1] == BS - 1 and c[0] + 1 in GROUPS:

@@ -10,7 +10,7 @@ P = 128
 T = 4
 MB = N // P
 CB = 2 * NOUT // P
-NU = BS * MB
+ROUNDS = BS * (MB // 2) * J
 
 F32 = mybir.dt.float32
 BF16 = mybir.dt.bfloat16
@@ -23,92 +23,86 @@ ACT = mybir.ActivationFunctionType
 
 FLOPS = 2 * BS * J * N * N * NF + 2 * BS * 2 * NOUT * KC * N
 
-CV_AT = (1, 1, 2, 1, 0, 2, 1, 0, 1, 0, 1, 2, 0)
-CV_ON_V = (10,)
-VEC_AT = 1
-X1_AT = 4
-SCB = 3
-SZ_AT = ((), (), (), (), (), (), (), (0,), (), (1,), (), (2,), ())
-ST_AT = ((), (), (), (), (), (), (), (), (), (), (), (), (3,))
-SZ2 = ((0, 1), (2,), (), (), (), (), (), (), (), ())
-SA2 = ((), (), (), (0,), (1, 2), (), (), (), (), ())
-GROUPS = (3, 6, 8)
-G_S = 5
-OPS = 5
-AHEAD = 5
-DRAIN = 2
-FINAL = "VGGVVVHGVGGVVVVV"
-FIN_AT = (1, 0, 1, 1, 2, 0, 2, 2, 3)
+BANKS = {"w": 2, "x1": 3, "turn": 2, "spare": 1}
+Y_BANKS = ("x1", "w", "spare", "x1", "w", "x1")
+CV_STEP = (0, 0, 1, 1, 5, 6, 7, 11, 11, 12, 12, 13)
+CV_ON_VECTOR = (7, 8)
+ZB = 3
+Z_ROUND = 7
 
 
 def tile_layer_simple_pa_kernel(
     tc, X, W_bytes, W_scale, N_batch, mask, cv1_w, cv1_b, cv2_w, cv2_b, bn_gamma, bn_beta, out
 ):
     nc = tc.nc
+    v = nc.vector
+    g = nc.gpsimd
     with ExitStack() as ctx:
         keep = ctx.enter_context(tc.tile_pool(name="keep", bufs=1))
         work = ctx.enter_context(tc.tile_pool(name="work", bufs=3))
-        psum = ctx.enter_context(tc.psum_pool(name="psum", bufs=3))
+        psum = ctx.enter_context(tc.psum_pool(name="psum", bufs=1))
         ctx.enter_context(tc.manual_schedule())
 
-        ws = keep.tile([P, T], F32)
-        nc.scalar.dma_start(out=ws[:], in_=W_scale[0, 0].rearrange("(p t) o -> p (t o)", t=T))
+        def bank(shape, dtype, name):
+            return psum.tile(shape, dtype, name=name, bufs=BANKS[name])
 
-        wb = [None] * NU
-        xs = [None] * BS
-        cvs = []
+        w_scale = keep.tile([P, T], F32)
+        nc.scalar.dma_start(out=w_scale[:], in_=W_scale[0, 0].rearrange("(p t) o -> p (t o)", t=T))
+
+        w_codes = []
+        x_rows = []
+        cv_rows = []
 
         def load_w(i):
             b, mb = divmod(i, MB)
-            t = keep.tile([P, N * J], U8, name=f"wb{i}")
+            codes = keep.tile([P, N * J], U8, name=f"w_codes{i}")
             nc.sync.dma_start(
-                out=t[:], in_=W_bytes[b].rearrange("(mb p) n j -> mb p (n j)", p=P)[mb]
+                out=codes[:], in_=W_bytes[b].rearrange("(mb p) n j -> mb p (n j)", p=P)[mb]
             )
-            wb[i] = t
+            w_codes.append(codes)
 
         def load_x(b):
-            t = keep.tile([P, T, N], BF16, name=f"xs{b}")
+            rows = keep.tile([P, T, N], BF16, name=f"x_rows{b}")
             for h in range(2):
                 nc.sync.dma_start(
-                    out=t[:, 2 * h : 2 * h + 2, :],
-                    in_=X[b].rearrange("(f t) n -> f t n", t=T)[:, 2 * h : 2 * h + 2, :],
+                    out=rows[:, 2 * h : 2 * h + 2, :],
+                    in_=X[b].rearrange("(p t) n -> p t n", t=T)[:, 2 * h : 2 * h + 2, :],
                 )
-            xs[b] = t
+            x_rows.append(rows)
 
         def load_cv(cb):
             src = cv2_w if cb < CB // 2 else cv1_w
-            t = keep.tile([P, KC], BF16, name=f"cvs{cb}")
+            rows = keep.tile([P, KC], BF16, name=f"cv_rows{cb}")
             r0 = (cb % (CB // 2)) * P
-            nc.sync.dma_start(out=t[:], in_=src[r0 : r0 + P, :])
-            cvs.append(t)
+            nc.sync.dma_start(out=rows[:], in_=src[r0 : r0 + P, :])
+            cv_rows.append(rows)
 
         ident_b = keep.tile([P, P], BF16)
         make_identity(nc, ident_b[:])
         ident_f = keep.tile([P, P], F32)
         make_identity(nc, ident_f[:])
-        mrow = keep.tile([P, BS * N], BF16)
-        vrow = keep.tile([P, P], BF16)
-        nc.gpsimd.memset(vrow[:], 0.0)
-        nc.gpsimd.memset(mrow[:], 0.0)
-        eps = keep.tile([P, 1], F32)
+        mask_row = keep.tile([P, BS * N], BF16)
+        vec_rows = keep.tile([P, P], BF16)
+        g.memset(vec_rows[:], 0.0)
+        g.memset(mask_row[:], 0.0)
         ones = keep.tile([P, P], BF16)
-        nc.gpsimd.memset(ones[:], 1.0)
+        g.memset(ones[:], 1.0)
 
         load_w(0)
         load_w(1)
-        load_x(0)
         load_w(2)
-        load_cv(0)
+        load_x(0)
         load_w(3)
+        load_cv(0)
         load_cv(1)
         for b in range(BS):
-            nc.sync.dma_start(out=mrow[0:1, b * N : (b + 1) * N], in_=mask[b])
-        nc.sync.dma_start(out=vrow[0:4, :], in_=cv2_b.rearrange("(r c) -> r c", c=P))
-        nc.sync.dma_start(out=vrow[4:8, :], in_=cv1_b.rearrange("(r c) -> r c", c=P))
-        nc.sync.dma_start(out=vrow[8:16, :], in_=bn_gamma.rearrange("(r c) -> r c", c=P))
-        nc.sync.dma_start(out=vrow[16:24, :], in_=bn_beta.rearrange("(r c) -> r c", c=P))
-        nbt = keep.tile([P, BS], BF16)
-        nc.sync.dma_start(out=nbt[:], in_=N_batch.partition_broadcast(P))
+            nc.sync.dma_start(out=mask_row[0:1, b * N : (b + 1) * N], in_=mask[b])
+        nc.sync.dma_start(out=vec_rows[0:4, :], in_=cv2_b.rearrange("(r c) -> r c", c=P))
+        nc.sync.dma_start(out=vec_rows[4:8, :], in_=cv1_b.rearrange("(r c) -> r c", c=P))
+        nc.sync.dma_start(out=vec_rows[8:16, :], in_=bn_gamma.rearrange("(r c) -> r c", c=P))
+        nc.sync.dma_start(out=vec_rows[16:24, :], in_=bn_beta.rearrange("(r c) -> r c", c=P))
+        counts = keep.tile([P, BS], BF16)
+        nc.sync.dma_start(out=counts[:], in_=N_batch.partition_broadcast(P))
         load_w(4)
         load_cv(2)
         load_x(1)
@@ -119,80 +113,89 @@ def tile_layer_simple_pa_kernel(
         for cb in range(4, CB):
             load_cv(cb)
 
-        warm = keep.tile([P, 1], F32)
-        nc.vector.memset(warm[:], 1.0)
-        warm2 = keep.tile([P, 1], F32)
-        nc.scalar.activation(out=warm2[:], in_=warm[:], func=ACT.Sqrt)
+        one = keep.tile([P, 1], F32)
+        v.memset(one[:], 1.0)
+        table = keep.tile([P, 1], F32)
+        nc.scalar.activation(out=table[:], in_=one[:], func=ACT.Abs_reciprocal_sqrt)
 
-        xq = [keep.tile([P, T * P], U32, name=f"xq{b}", align_bytes=64) for b in range(BS)]
-        xsc = [keep.tile([P, T * P], U8, name=f"xsc{b}", align_bytes=64) for b in range(BS)]
-        xg = {}
+        zeros = keep.tile([P, N], BF16)
+        v.memset(zeros[:], 0.0)
+
+        def idle_matmul():
+            ps = bank([P, N], F32, "spare")
+            nc.tensor.matmul(ps[:], lhsT=zeros[:, 0:P], rhs=zeros[:], start=True, stop=True)
+
+        x_q = [keep.tile([P, T * P], U32, name=f"x_q{b}", align_bytes=64) for b in range(BS)]
+        x_s = [keep.tile([P, T * P], U8, name=f"x_s{b}", align_bytes=64) for b in range(BS)]
+        x_t = {}
 
         def x_turn(b):
-            xg[b] = work.tile([P, T * P * T], BF16, name="xg", align_bytes=64)
-            words = xs[b][:].bitcast(F32).rearrange("p t (q u) -> p t u q", u=2)
+            x_t[b] = work.tile([P, T * P * T], BF16, name="x_t", bufs=2, align_bytes=64)
+            pairs = x_rows[b][:].bitcast(F32).rearrange("p t (q u) -> p t u q", u=2)
             for h in range(2):
-                ps = psum.tile([P, 2, 2, P], F32, name="y")
+                ps = bank([P, 2, 2, P], F32, "turn")
                 for i in range(2):
                     for u in range(2):
-                        nc.tensor.transpose(ps[:, i, u, :], words[:, 2 * h + i, u, :], ident_f[:])
+                        nc.tensor.transpose(ps[:, i, u, :], pairs[:, 2 * h + i, u, :], ident_f[:])
+                half = x_t[b][:, h * 1024 : (h + 1) * 1024].bitcast(F32)
                 nc.scalar.copy(
-                    out=xg[b][:, h * 1024 : (h + 1) * 1024].bitcast(F32).rearrange("p (i f u) -> p i f u", i=2, u=2),
-                    in_=ps[:].rearrange("p i u f -> p i f u"),
+                    out=half.rearrange("p (i f u) -> p i f u", i=2, u=2), in_=ps[:].rearrange("p i u f -> p i f u")
                 )
 
         def x_quant(b):
-            nc.vector.quantize_mx(out=xq[b][:].bitcast(FP8X4), scales=xsc[b][:], in_=xg[b][:])
+            v.quantize_mx(out=x_q[b][:].bitcast(FP8X4), scales=x_s[b][:], in_=x_t[b][:])
 
-        cvq = keep.tile([P, CB * J, P], U32, align_bytes=64)
-        cvsc = keep.tile([P, CB * J, P], U8, align_bytes=64)
-        cvg = {}
-        cps = {}
+        cv_q = keep.tile([P, CB * J, P], U32, align_bytes=64)
+        cv_s = keep.tile([P, CB * J, P], U8, align_bytes=64)
+        cv_t = {}
 
         def cv_turn(h):
             if h % 2 == 0:
-                cvg[h // 2] = work.tile([P, 4 * P * T], BF16, name="cvg", align_bytes=64)
-            cps[h] = psum.tile([P, 2, 2, P], F32, name="y")
+                cv_t[h // 2] = work.tile([P, 4 * P * T], BF16, name="cv_t", bufs=2, align_bytes=64)
+            ps = bank([P, 2, 2, P], F32, "turn")
             for i in range(2):
-                cb, g = divmod(2 * h + i, J)
-                words = cvs[cb][:].bitcast(F32).rearrange("p (g q u) -> p g u q", g=J, u=2)
+                cb, j = divmod(2 * h + i, J)
+                pairs = cv_rows[cb][:].bitcast(F32).rearrange("p (j q u) -> p j u q", j=J, u=2)
                 for u in range(2):
-                    nc.tensor.transpose(cps[h][:, i, u, :], words[:, g, u, :], ident_f[:])
-
-        def cv_copy(h):
+                    nc.tensor.transpose(ps[:, i, u, :], pairs[:, j, u, :], ident_f[:])
             o = (h % 2) * 1024
-            dst = cvg[h // 2][:, o : o + 1024].bitcast(F32).rearrange("p (i f u) -> p i f u", i=2, u=2)
-            src = cps[h][:].rearrange("p i u f -> p i f u")
-            if h in CV_ON_V:
-                nc.vector.tensor_copy(out=dst, in_=src)
+            dst = cv_t[h // 2][:, o : o + 1024].bitcast(F32).rearrange("p (i c u) -> p i c u", i=2, u=2)
+            src = ps[:].rearrange("p i u c -> p i c u")
+            if h in CV_ON_VECTOR:
+                v.tensor_copy(out=dst, in_=src)
             else:
                 nc.scalar.copy(out=dst, in_=src)
 
-        def cv_quant(h):
-            s4 = 4 * h
-            nc.vector.quantize_mx(
-                out=cvq[:, s4 : s4 + 4, :].rearrange("p g c -> p (g c)").bitcast(FP8X4),
-                scales=cvsc[:, s4 : s4 + 4, :].rearrange("p g c -> p (g c)"),
-                in_=cvg[h][:],
-            )
+        def cv_turns(step):
+            for h in range(len(CV_STEP)):
+                if CV_STEP[h] == step:
+                    cv_turn(h)
 
-        x1g = [keep.tile([P, J, N * T], BF16, name=f"x1g{b}", align_bytes=64) for b in range(BS)]
-        x1q = [keep.tile([P, J, N], U32, name=f"x1q{b}", align_bytes=64) for b in range(BS)]
-        x1s = [keep.tile([P, J, N], U8, name=f"x1s{b}", align_bytes=64) for b in range(BS)]
-        ws_b = ws[:].rearrange("p (u e) -> p u e", u=2).unsqueeze(1).to_broadcast([P, 2 * P, 2, 2])
-        one = keep.tile([P, 1], F32)
-        nc.vector.memset(one[:], 1.0)
-        wf = {}
-        wg = {}
-        wt = {}
-        wq = {}
-        mm = {}
+        def cv_quants(step):
+            for h in range(1, len(CV_STEP), 2):
+                if CV_STEP[h] == step - 1:
+                    four = slice(2 * h - 2, 2 * h + 2)
+                    v.quantize_mx(
+                        out=cv_q[:, four, :].rearrange("p g c -> p (g c)").bitcast(FP8X4),
+                        scales=cv_s[:, four, :].rearrange("p g c -> p (g c)"),
+                        in_=cv_t[h // 2][:],
+                    )
+
+        x1_t = [keep.tile([P, J, N * T], BF16, name=f"x1_t{b}", align_bytes=64) for b in range(BS)]
+        x1_q = [keep.tile([P, J, N], U32, name=f"x1_q{b}", align_bytes=64) for b in range(BS)]
+        x1_s = [keep.tile([P, J, N], U8, name=f"x1_s{b}", align_bytes=64) for b in range(BS)]
+        scale_words = w_scale[:].rearrange("p (u e) -> p u e", u=2).unsqueeze(1).to_broadcast([P, 2 * P, 2, 2])
+        w_wide = {}
+        w_banks = {}
+        w_t = {}
+        w_q = {}
+        x1_banks = {}
 
         def widen(i):
-            wf[i] = work.tile([P, J, N], BF16, name="wf", bufs=4)
-            nc.vector.tensor_scalar(
-                out=wf[i][:].rearrange("p j n -> p n j"),
-                in0=wb[i][:].rearrange("p (n j) -> p n j", j=J).bitcast(FP8),
+            w_wide[i] = work.tile([P, J, N], BF16, name="w_wide", bufs=6)
+            v.tensor_scalar(
+                out=w_wide[i][:].rearrange("p j n -> p n j"),
+                in0=w_codes[i][:].rearrange("p (n j) -> p n j", j=J).bitcast(FP8),
                 scalar1=one[:],
                 scalar2=None,
                 op0=ALU.mult,
@@ -200,39 +203,40 @@ def tile_layer_simple_pa_kernel(
 
         def w_turn(r):
             s, j = divmod(r, J)
-            wt[r] = psum.tile([P, 2, 2 * P], F32, name="tw", bufs=2)
+            w_banks[r] = bank([P, 2, 2 * P], F32, "w")
             for h in range(2):
-                words = wf[2 * s + h][:, j, :].bitcast(F32).rearrange("p (q u) -> p u q", u=2)
-                for e in range(2):
-                    nc.tensor.transpose(wt[r][:, e, h * P : (h + 1) * P], words[:, e, :], ident_f[:])
+                pairs = w_wide[2 * s + h][:, j, :].bitcast(F32).rearrange("p (q u) -> p u q", u=2)
+                for u in range(2):
+                    nc.tensor.transpose(w_banks[r][:, u, h * P : (h + 1) * P], pairs[:, u, :], ident_f[:])
 
-        def w_scale(r):
-            wg[r] = work.tile([P, 2 * P * T], BF16, name="wg", align_bytes=64)
-            nc.vector.tensor_tensor(
-                out=wg[r][:].rearrange("p (m u e) -> p m u e", u=2, e=2),
-                in0=wt[r][:].rearrange("p u m -> p (u m)").bitcast(BF16).rearrange("p (u m e) -> p m u e", u=2, e=2),
-                in1=ws_b,
+        def w_product(r):
+            w_t[r] = work.tile([P, 2 * P * T], BF16, name="w_t", align_bytes=64)
+            values = w_banks[r][:].rearrange("p u m -> p (u m)").bitcast(BF16)
+            v.tensor_tensor(
+                out=w_t[r][:].rearrange("p (m u e) -> p m u e", u=2, e=2),
+                in0=values.rearrange("p (u m e) -> p m u e", u=2, e=2),
+                in1=scale_words,
                 op=ALU.mult,
             )
 
         def w_quant(r):
-            q = work.tile([P, 2 * P], U32, name="wq", align_bytes=64)
-            s = work.tile([P, 2 * P], U8, name="wsc", align_bytes=64)
-            nc.vector.quantize_mx(out=q[:].bitcast(FP8X4), scales=s[:], in_=wg[r][:])
-            wq[r] = (q, s)
+            q = work.tile([P, 2 * P], U32, name="w_q", align_bytes=64)
+            s = work.tile([P, 2 * P], U8, name="w_s", align_bytes=64)
+            v.quantize_mx(out=q[:].bitcast(FP8X4), scales=s[:], in_=w_t[r][:])
+            w_q[r] = (q, s)
 
         def step1(r, h):
-            s, j = divmod(r, J)
-            b = s // 2
-            q, sc = wq[r]
-            mm[r, h] = psum.tile([P, T, P], F32, name="mm", bufs=3)
+            b = r // (2 * J)
+            q, s = w_q[r]
+            nodes = slice(h * P, (h + 1) * P)
+            x1_banks[r, h] = bank([P, T, P], F32, "x1")
             for t in range(T):
                 nc.tensor.matmul_mx(
-                    out=mm[r, h][:, t, :],
-                    lhsT=xq[b][:, t * P : (t + 1) * P].bitcast(FP8X4),
-                    lhsT_scale=xsc[b][:, t * P : (t + 1) * P],
-                    rhs=q[:, h * P : (h + 1) * P].bitcast(FP8X4),
-                    rhs_scale=sc[:, h * P : (h + 1) * P],
+                    out=x1_banks[r, h][:, t, :],
+                    lhsT=x_q[b][:, t * P : (t + 1) * P].bitcast(FP8X4),
+                    lhsT_scale=x_s[b][:, t * P : (t + 1) * P],
+                    rhs=q[:, nodes].bitcast(FP8X4),
+                    rhs_scale=s[:, nodes],
                     start=True,
                     stop=True,
                 )
@@ -241,16 +245,18 @@ def tile_layer_simple_pa_kernel(
             s, j = divmod(r, J)
             c0 = (2 * (s % 2) + h) * P * T
             nc.scalar.copy(
-                out=x1g[s // 2][:, j, c0 : c0 + P * T].rearrange("p (m t) -> p m t", t=T),
-                in_=mm[r, h][:].rearrange("p t m -> p m t"),
+                out=x1_t[s // 2][:, j, c0 : c0 + P * T].rearrange("p (m t) -> p m t", t=T),
+                in_=x1_banks[r, h][:].rearrange("p t m -> p m t"),
             )
 
-        def x1_quant(b, h, j):
-            c0 = h * 2 * P
-            nc.vector.quantize_mx(
-                out=x1q[b][:, j, c0 : c0 + 2 * P].bitcast(FP8X4),
-                scales=x1s[b][:, j, c0 : c0 + 2 * P],
-                in_=x1g[b][:, j, c0 * T : (c0 + 2 * P) * T],
+        def x1_quant(r):
+            s, j = divmod(r, J)
+            b = s // 2
+            c0 = (s % 2) * 2 * P
+            v.quantize_mx(
+                out=x1_q[b][:, j, c0 : c0 + 2 * P].bitcast(FP8X4),
+                scales=x1_s[b][:, j, c0 : c0 + 2 * P],
+                in_=x1_t[b][:, j, c0 * T : (c0 + 2 * P) * T],
             )
 
         vec = keep.tile([P, 3 * CB], F32)
@@ -258,258 +264,320 @@ def tile_layer_simple_pa_kernel(
         gamma = vec[:, CB : 2 * CB]
         beta = vec[:, 2 * CB : 3 * CB]
         mk = keep.tile([P, BS, N], F32)
-        msum = keep.tile([P, BS], F32)
-        nbias = keep.tile([P, CB], F32)
-        tot = keep.tile([P, 1], F32)
-        rt = keep.tile([P, 1], F32)
-        mtot = keep.tile([P, 1], F32)
-        mr1 = keep.tile([P, 1], F32)
-        bm1 = keep.tile([P, CB], F32)
+        mask_sums = keep.tile([P, BS], F32)
+        eps = keep.tile([P, 1], F32)
+        neg_bias = keep.tile([P, CB], F32)
+        total = keep.tile([P, 1], F32)
+        rtotal = keep.tile([P, 1], F32)
+        mask_sum = keep.tile([P, 1], F32)
+        ratio1 = keep.tile([P, 1], F32)
+        shift = keep.tile([P, CB], F32)
         c1 = keep.tile([P, 1], F32)
+        c1r = keep.tile([P, 1], F32)
         c2 = keep.tile([P, CB], F32)
+        c3 = keep.tile([P, CB], F32)
+
+        def mask_bank(b):
+            ps = bank([P, N], F32, "turn")
+            nc.tensor.matmul(
+                ps[:], lhsT=ones[:], rhs=mask_row[:, b * N : (b + 1) * N], start=True, stop=True
+            )
+            return ps
 
         def vectors():
-            pv = psum.tile([P, P], BF16, name="y")
-            nc.tensor.transpose(pv[:], vrow[:], ident_b[:])
-            nc.vector.tensor_copy(out=vec[:], in_=pv[:, 0 : 3 * CB])
+            ps = bank([P, P], BF16, "turn")
+            nc.tensor.transpose(ps[:], vec_rows[:], ident_b[:])
+            v.tensor_copy(out=vec[:], in_=ps[:, 0 : 3 * CB])
             for b in range(BS):
-                pm = psum.tile([P, N], F32, name="y")
-                nc.tensor.matmul(pm[:], lhsT=ones[:], rhs=mrow[:, b * N : (b + 1) * N], start=True, stop=True)
-                nc.scalar.activation(out=mk[:, b, :], in_=pm[:], func=ACT.Copy, accum_out=msum[:, b : b + 1])
-            nc.gpsimd.tensor_tensor(out=tot[:], in0=nbt[:, 0:1], in1=nbt[:, 1:2], op=ALU.add)
-            nc.gpsimd.tensor_scalar(out=eps[:], in0=tot[:], scalar1=0.0, scalar2=EPS, op0=ALU.mult, op1=ALU.add)
-            nc.gpsimd.tensor_scalar(out=nbias[:], in0=bias, scalar1=-1.0, scalar2=0.0, op0=ALU.mult, op1=ALU.add)
-            nc.vector.reciprocal(out=rt[:], in_=tot[:])
-            nc.gpsimd.tensor_tensor(out=mtot[:], in0=msum[:, 0:1], in1=msum[:, 1:2], op=ALU.add)
-            nc.gpsimd.tensor_scalar(out=mr1[:], in0=mtot[:], scalar1=rt[:], scalar2=1.0, op0=ALU.mult, op1=ALU.subtract)
-            nc.gpsimd.memset(bm1[:, 0:SCB], 0.0)
-            nc.gpsimd.tensor_scalar(out=bm1[:, SCB:], in0=bias[:, SCB:], scalar1=mr1[:], scalar2=0.0, op0=ALU.mult, op1=ALU.add)
-            nc.gpsimd.tensor_scalar(out=c1[:], in0=tot[:], scalar1=-2.0, scalar2=mtot[:], op0=ALU.mult, op1=ALU.add)
-            nc.gpsimd.tensor_scalar(out=c2[:], in0=bm1[:], scalar1=tot[:], scalar2=2.0, op0=ALU.mult, op1=ALU.mult)
+                nc.scalar.activation(
+                    out=mk[:, b, :], in_=mask_bank(b)[:], func=ACT.Copy, accum_out=mask_sums[:, b : b + 1]
+                )
+            g.tensor_tensor(out=total[:], in0=counts[:, 0:1], in1=counts[:, 1:2], op=ALU.add)
+            g.tensor_scalar(out=eps[:], in0=total[:], scalar1=0.0, scalar2=EPS, op0=ALU.mult, op1=ALU.add)
+            g.tensor_scalar(out=neg_bias[:], in0=bias, scalar1=-1.0, scalar2=0.0, op0=ALU.mult, op1=ALU.add)
+            v.reciprocal(out=rtotal[:], in_=total[:])
+            g.tensor_tensor(out=mask_sum[:], in0=mask_sums[:, 0:1], in1=mask_sums[:, 1:2], op=ALU.add)
+            g.tensor_scalar(
+                out=ratio1[:], in0=mask_sum[:], scalar1=rtotal[:], scalar2=1.0, op0=ALU.mult, op1=ALU.subtract
+            )
+            g.memset(shift[:, 0:ZB], 0.0)
+            g.tensor_scalar(
+                out=shift[:, ZB:], in0=bias[:, ZB:], scalar1=ratio1[:], scalar2=0.0, op0=ALU.mult, op1=ALU.add
+            )
+            g.tensor_scalar(
+                out=c1[:], in0=total[:], scalar1=-2.0, scalar2=mask_sum[:], op0=ALU.mult, op1=ALU.add
+            )
+            g.tensor_scalar(out=c2[:], in0=shift[:], scalar1=total[:], scalar2=2.0, op0=ALU.mult, op1=ALU.mult)
+            g.tensor_tensor(out=c1r[:], in0=rtotal[:], in1=c1[:], op=ALU.mult)
+            g.tensor_scalar(out=c3[:], in0=shift[:], scalar1=c1[:], scalar2=0.0, op0=ALU.mult, op1=ALU.add)
+            g.tensor_tensor(out=c3[:], in0=c3[:], in1=c2[:], op=ALU.add)
 
-        st = keep.tile([P, 2, BS, CB], F32)
-        u = {}
-        ys = {}
-        sms = {}
+        sums = keep.tile([P, 2, BS, CB], F32)
+        y_banks = {}
+        kept = {}
+        squares = {}
 
-        def conv(cb, b, tag):
-            ys[cb, b] = psum.tile([P, N], F32, name=tag, bufs=2 if tag == "tw" else 3)
+        def conv(cb, b, name):
+            y_banks[cb, b] = bank([P, N], F32, name)
             for j in range(J):
                 nc.tensor.matmul_mx(
-                    out=ys[cb, b][:],
-                    lhsT=cvq[:, cb * J + j, :].bitcast(FP8X4),
-                    lhsT_scale=cvsc[:, cb * J + j, :],
-                    rhs=x1q[b][:, j, :].bitcast(FP8X4),
-                    rhs_scale=x1s[b][:, j, :],
+                    out=y_banks[cb, b][:],
+                    lhsT=cv_q[:, cb * J + j, :].bitcast(FP8X4),
+                    lhsT_scale=cv_s[:, cb * J + j, :],
+                    rhs=x1_q[b][:, j, :].bitcast(FP8X4),
+                    rhs_scale=x1_s[b][:, j, :],
                     start=(j == 0),
                     stop=(j == J - 1),
                 )
 
         def stat1(cb, b):
-            ub = work.tile([P, N], F32, name="u", bufs=16)
-            nc.vector.scalar_tensor_tensor(
-                out=ub[:], in0=ys[cb, b][:], scalar=nbias[:, cb : cb + 1], in1=mk[:, b, :],
-                op0=ALU.max, op1=ALU.mult, accum_out=st[:, 0, b, cb : cb + 1],
+            kept[cb, b] = work.tile([P, N], F32, name="kept", bufs=2 * CB)
+            v.scalar_tensor_tensor(
+                out=kept[cb, b][:], in0=y_banks[cb, b][:], scalar=neg_bias[:, cb : cb + 1], in1=mk[:, b, :],
+                op0=ALU.max, op1=ALU.mult, accum_out=sums[:, 0, b, cb : cb + 1],
             )
-            u[cb, b] = ub
 
         def stat2(cb, b):
-            junk = work.tile([P, N], F32, name="junk", bufs=2)
-            nc.vector.scalar_tensor_tensor(
-                out=junk[:], in0=ys[cb, b][:], scalar=nbias[:, cb : cb + 1], in1=u[cb, b][:],
-                op0=ALU.max, op1=ALU.mult, accum_out=st[:, 1, b, cb : cb + 1],
+            unread = work.tile([P, N], F32, name="unread_v", bufs=2)
+            v.scalar_tensor_tensor(
+                out=unread[:], in0=y_banks[cb, b][:], scalar=neg_bias[:, cb : cb + 1], in1=kept[cb, b][:],
+                op0=ALU.max, op1=ALU.mult, accum_out=sums[:, 1, b, cb : cb + 1],
             )
 
-        g = nc.gpsimd
-        v = nc.vector
-        s12 = keep.tile([P, 2, CB], F32)
-        dd = keep.tile([P, CB], F32)
-        qq = keep.tile([P, CB], F32)
-        vv = keep.tile([P, CB], F32)
-        ww = keep.tile([P, CB], F32)
-        sd = keep.tile([P, CB], F32)
-        rs = keep.tile([P, CB], F32)
-        aa = keep.tile([P, CB], F32)
-        ad = keep.tile([P, CB], F32)
-        nb = keep.tile([P, CB], F32)
-
-        def norm_ops(lo, hi):
-            c = slice(lo, hi)
-            return [
-                lambda: v.tensor_tensor(out=s12[:, :, c], in0=st[:, :, 0, c], in1=st[:, :, 1, c], op=ALU.add),
-                lambda: v.scalar_tensor_tensor(out=dd[:, c], in0=s12[:, 0, c], scalar=rt[:], in1=bm1[:, c], op0=ALU.mult, op1=ALU.add),
-                lambda: v.scalar_tensor_tensor(out=qq[:, c], in0=dd[:, c], scalar=c1[:], in1=c2[:, c], op0=ALU.mult, op1=ALU.add),
-                lambda: v.tensor_tensor(out=vv[:, c], in0=dd[:, c], in1=qq[:, c], op=ALU.mult),
-                lambda: (
-                    v.tensor_tensor(out=ww[:, c], in0=vv[:, c], in1=s12[:, 1, c], op=ALU.add),
-                    nc.scalar.activation(out=sd[:, c], in_=ww[:, c], func=ACT.Sqrt, scale=rt[:], bias=eps[:]),
-                ),
-                lambda: v.reciprocal(out=rs[:, c], in_=sd[:, c]),
-                lambda: v.tensor_tensor(out=aa[:, c], in0=rs[:, c], in1=gamma[:, c], op=ALU.mult),
-                lambda: v.tensor_tensor(out=ad[:, c], in0=aa[:, c], in1=dd[:, c], op=ALU.mult),
-                lambda: (v.tensor_tensor(out=nb[:, c], in0=ad[:, c], in1=beta[:, c], op=ALU.subtract), range(lo, hi))[1],
-            ]
-
-        fin = {}
-
-        sz = {}
-
-        def z_pass(cb, b):
-            z = work.tile([P, N], F32, name="z", bufs=2)
-            nc.scalar.activation(out=z[:], in_=ys[cb, b][:], func=ACT.Relu, bias=bias[:, cb : cb + 1])
-            ub = work.tile([P, N], F32, name="u", bufs=16)
-            g.tensor_tensor(out=ub[:], in0=z[:], in1=mk[:, b, :], op=ALU.mult)
-            q = work.tile([P, N], F32, name="q", bufs=2)
-            g.tensor_tensor(out=q[:], in0=z[:], in1=ub[:], op=ALU.mult)
-            u[cb, b] = ub
-            sz[cb, b] = q
+        def z_products(cb, b):
+            z = work.tile([P, N], F32, name="kept", bufs=2 * CB)
+            nc.scalar.activation(out=z[:], in_=y_banks[cb, b][:], func=ACT.Relu, bias=bias[:, cb : cb + 1])
+            zm = work.tile([P, N], F32, name="zm", bufs=3)
+            g.tensor_tensor(out=zm[:], in0=z[:], in1=mk[:, b, :], op=ALU.mult)
+            zzm = work.tile([P, N], F32, name="zzm", bufs=3)
+            g.tensor_tensor(out=zzm[:], in0=z[:], in1=zm[:], op=ALU.mult)
+            kept[cb, b] = z
+            squares[cb, b] = (zm, zzm)
 
         def z_sums(cb, b):
-            for i, t in enumerate((u[cb, b], sz[cb, b])):
-                junk = work.tile([P, N], F32, name="junks", bufs=2)
-                nc.scalar.activation(out=junk[:], in_=t[:], func=ACT.Copy, accum_out=st[:, i, b, cb : cb + 1])
+            for i, product in enumerate(squares[cb, b]):
+                unread = work.tile([P, N], F32, name="unread_s", bufs=2)
+                nc.scalar.activation(
+                    out=unread[:], in_=product[:], func=ACT.Copy, accum_out=sums[:, i, b, cb : cb + 1]
+                )
 
-        def finish_s(cb, b):
-            na = aa[:, cb : cb + 1]
-            nbc = nb[:, cb : cb + 1]
-            kind = FINAL[2 * cb + b]
-            bm = work.tile([P, N], F32, name="bm", bufs=4)
-            au = None
-            if kind == "H":
-                g.tensor_scalar(out=bm[:], in0=mk[:, b, :], scalar1=nbc, scalar2=0.0, op0=ALU.mult, op1=ALU.add)
-            else:
-                nc.scalar.activation(out=bm[:], in_=mk[:, b, :], func=ACT.Copy, scale=nbc)
-            if kind != "V":
-                au = work.tile([P, N], F32, name="au", bufs=4)
-                nc.scalar.activation(out=au[:], in_=u[cb, b][:], func=ACT.Copy, scale=na)
-            fin[cb, b] = (bm, au)
+        both = keep.tile([P, 2, CB], F32)
+        d = keep.tile([P, CB], F32)
+        c1d_c2 = keep.tile([P, CB], F32)
+        var_part = keep.tile([P, CB], F32)
+        var_sum = keep.tile([P, CB], F32)
+        neg_gd = keep.tile([P, CB], F32)
+        rstd = keep.tile([P, CB], F32)
+        neg_fd = keep.tile([P, CB], F32)
+        factor = keep.tile([P, CB], F32)
+        offset = keep.tile([P, CB], F32)
 
-        def finish(cb, b):
-            bm, au = fin[cb, b]
-            o = work.tile([P, N], F32, name="o", bufs=8)
-            if au is None:
-                nc.vector.scalar_tensor_tensor(
-                    out=o[:], in0=u[cb, b][:], scalar=aa[:, cb : cb + 1], in1=bm[:], op0=ALU.mult, op1=ALU.subtract
+        def norm_steps(lo, hi):
+            c = slice(lo, hi)
+
+            def add_graphs():
+                v.tensor_tensor(out=both[:, :, c], in0=sums[:, :, 0, c], in1=sums[:, :, 1, c], op=ALU.add)
+
+            def means():
+                v.scalar_tensor_tensor(
+                    out=d[:, c], in0=both[:, 0, c], scalar=rtotal[:], in1=shift[:, c], op0=ALU.mult, op1=ALU.add
+                )
+                v.scalar_tensor_tensor(
+                    out=c1d_c2[:, c], in0=both[:, 0, c], scalar=c1r[:], in1=c3[:, c], op0=ALU.mult, op1=ALU.add
+                )
+
+            def products():
+                v.tensor_tensor(out=var_part[:, c], in0=d[:, c], in1=c1d_c2[:, c], op=ALU.mult)
+                v.scalar_tensor_tensor(
+                    out=neg_gd[:, c], in0=d[:, c], scalar=-1.0, in1=gamma[:, c], op0=ALU.mult, op1=ALU.mult
+                )
+
+            def roots():
+                v.tensor_tensor(out=var_sum[:, c], in0=var_part[:, c], in1=both[:, 1, c], op=ALU.add)
+                nc.scalar.activation(
+                    out=rstd[:, c], in_=var_sum[:, c], func=ACT.Abs_reciprocal_sqrt, scale=rtotal[:], bias=eps[:]
+                )
+
+            def factors():
+                v.tensor_tensor(out=neg_fd[:, c], in0=rstd[:, c], in1=neg_gd[:, c], op=ALU.mult)
+                v.tensor_tensor(out=factor[:, c], in0=rstd[:, c], in1=gamma[:, c], op=ALU.mult)
+
+            def offsets():
+                v.tensor_tensor(out=offset[:, c], in0=neg_fd[:, c], in1=beta[:, c], op=ALU.add)
+                ready.extend((cb, b) for cb in range(lo, hi) for b in range(BS))
+
+            return [add_graphs, means, products, roots, None, factors, offsets]
+
+        last = CB - 1
+        l_sum, l_d, l_c1d_c2, l_var, l_var_eps, l_neg_gd, l_rstd = (
+            keep.tile([P, 1], F32, name=f"last{i}") for i in range(7)
+        )
+
+        def last_norm_steps():
+            c = slice(last, CB)
+
+            def add_graphs():
+                v.tensor_tensor(out=l_sum[:], in0=sums[:, 0, 0, c], in1=sums[:, 0, 1, c], op=ALU.add)
+
+            def means():
+                v.tensor_scalar(
+                    out=l_d[:], in0=l_sum[:], scalar1=rtotal[:], scalar2=shift[:, c], op0=ALU.mult, op1=ALU.add
+                )
+                v.tensor_scalar(
+                    out=l_c1d_c2[:], in0=l_sum[:], scalar1=c1r[:], scalar2=c3[:, c], op0=ALU.mult, op1=ALU.add
+                )
+
+            def products():
+                v.scalar_tensor_tensor(
+                    out=l_var[:], in0=l_d[:], scalar=l_c1d_c2[:], in1=sums[:, 1, 0, c], op0=ALU.mult, op1=ALU.add
+                )
+                v.scalar_tensor_tensor(
+                    out=l_neg_gd[:], in0=l_d[:], scalar=-1.0, in1=gamma[:, c], op0=ALU.mult, op1=ALU.mult
+                )
+
+            def add_eps():
+                v.tensor_scalar(
+                    out=l_var_eps[:], in0=l_var[:], scalar1=rtotal[:], scalar2=EPS, op0=ALU.mult, op1=ALU.add
+                )
+
+            def root():
+                nc.scalar.activation(
+                    out=l_rstd[:], in_=sums[:, 1, 1, c], func=ACT.Abs_reciprocal_sqrt, scale=rtotal[:], bias=l_var_eps[:]
+                )
+
+            def factors():
+                v.scalar_tensor_tensor(
+                    out=offset[:, c], in0=l_rstd[:], scalar=l_neg_gd[:], in1=beta[:, c], op0=ALU.mult, op1=ALU.add
+                )
+                v.tensor_tensor(out=factor[:, c], in0=l_rstd[:], in1=gamma[:, c], op=ALU.mult)
+                ready.extend((last, b) for b in range(BS))
+
+            return [add_graphs, means, products, add_eps, root, None, factors]
+
+        mask_banks = []
+        scaled = {}
+
+        def scale(cb, b):
+            scaled[cb, b] = work.tile([P, N], F32, name="scaled", bufs=5)
+            f = factor[:, cb : cb + 1]
+            if cb < ZB:
+                nc.scalar.activation(
+                    out=scaled[cb, b][:], in_=kept[cb, b][:], func=ACT.Identity, scale=f, bias=offset[:, cb : cb + 1]
                 )
             else:
-                g.tensor_tensor(out=o[:], in0=au[:], in1=bm[:], op=ALU.subtract)
+                nc.scalar.activation(out=scaled[cb, b][:], in_=kept[cb, b][:], func=ACT.Copy, scale=f)
+
+        def finish(cb, b):
+            o = work.tile([P, N], F32, name="o", bufs=7)
+            if cb < ZB:
+                v.tensor_tensor(out=o[:], in0=mask_banks[b][:], in1=scaled[cb, b][:], op=ALU.mult)
+            else:
+                v.scalar_tensor_tensor(
+                    out=o[:], in0=mask_banks[b][:], scalar=offset[:, cb : cb + 1], in1=scaled[cb, b][:],
+                    op0=ALU.mult, op1=ALU.add,
+                )
             nc.sync.dma_start(out=out[b, cb * P : (cb + 1) * P, :], in_=o[:])
 
-        cv_done = [0]
-
-        def cv_banks(n):
-            hs = list(range(cv_done[0], cv_done[0] + n))
-            cv_done[0] += n
-            return hs
-
-        def stats(c):
-            stat1(*c)
-            stat2(*c)
-
-        R = BS * J * MB // 2
-        cvh = []
-        szs = []
-        widen(0)
-        widen(1)
+        for i in range(3):
+            widen(i)
         w_turn(0)
         x_turn(0)
-        for r in range(R + 1):
-            hs = cv_banks(CV_AT[r])
+        for r in range(ROUNDS + 1):
             if r == 1:
                 x_quant(0)
+            if r + 1 < ROUNDS:
+                w_turn(r + 1)
             if r > 0:
                 w_quant(r - 1)
                 for h in range(2):
                     step1(r - 1, h)
                     x1_copy(r - 1, h)
-            if r < R:
-                w_scale(r)
-            if r % J and r + J - r % J < R:
-                widen(2 * (r // J + 1) + r % J - 1)
-            if r + 1 < R:
-                w_turn(r + 1)
-            if r == X1_AT:
+            if r in (3, 5, 7, 9):
+                idle_matmul()
+            if r < ROUNDS:
+                w_product(r)
+            if r in (0, 1, 3, 5, 7):
+                widen(3 + (r + 1) // 2)
+            if r == 3:
                 x_turn(1)
-            if r == X1_AT + 1:
+            if r == 4:
                 x_quant(1)
-            if r == VEC_AT:
                 vectors()
-            for h in hs:
-                cv_turn(h)
-                cv_copy(h)
+            cv_turns(r)
             if r >= 2:
-                s, j = divmod(r - 2, J)
-                x1_quant(s // 2, s % 2, j)
-            for h in cvh:
-                if h % 2 == 1:
-                    cv_quant(h // 2)
-            cvh = hs
-            for cb in ST_AT[r]:
-                conv(cb, 0, "y")
-                stats((cb, 0))
-            for c in szs:
-                z_sums(*c)
-            szs = [(cb, 0) for cb in SZ_AT[r]]
-            for c in szs:
-                conv(*c, "y")
-                z_pass(*c)
-        for h in cvh:
-            if h % 2 == 1:
-                cv_quant(h // 2)
-        x1_quant(1, 1, J - 1)
+                x1_quant(r - 2)
+            cv_quants(r)
+            cb, odd = divmod(r - Z_ROUND, 2)
+            if odd == 0 and 1 <= cb <= ZB:
+                z_sums(cb - 1, 0)
+            if odd == 0 and 0 <= cb < ZB:
+                conv(cb, 0, "spare")
+                z_products(cb, 0)
+        x1_quant(ROUNDS - 1)
+        z_sums(ZB - 1, 0)
 
-        done = [(cb, 0) for k in range(R + 1) for cb in ST_AT[k]]
-        todo = [(cb, b) for cb in range(CB) for b in range(BS) if cb >= SCB and (cb, b) not in done]
-        seq = []
-        for i, c in enumerate(todo):
-            seq += [(cb, 1) for cb in SZ2[i]] + [c]
-        tags = ("y", "mm", "tw", "y", "mm", "tw", "y", "mm")
-        ahead = [0]
+        blocks = [(cb, b) for cb in range(ZB, CB) for b in range(BS)]
+        order = []
+        for i in range(len(blocks)):
+            if i % 2 == 0 and i // 2 < ZB:
+                order.append((i // 2, 1))
+            order.append(blocks[i])
+        issued = []
 
-        def conv_next(n):
-            for i in range(ahead[0], min(ahead[0] + n, len(seq))):
-                conv(*seq[i], tags[i % 8])
-            ahead[0] += n
+        def convs(n):
+            for cb, b in order[len(issued) : len(issued) + n]:
+                conv(cb, b, Y_BANKS[len(issued) % len(Y_BANKS)])
+                issued.append((cb, b))
 
-        for c in szs:
-            z_sums(*c)
-        wait = []
-        ops = []
-        start = SCB
-        conv_next(AHEAD)
+        chains = []
+        ready = []
 
-        def norm_some(n):
-            for op in ops[:n]:
-                done_now = op()
-                if isinstance(done_now, range):
-                    wait.extend((cb, b) for cb in done_now for b in range(BS))
-            return ops[n:]
+        def small_steps():
+            for chain in list(chains):
+                if chain[0] is not None:
+                    chain[0]()
+                chain[:] = chain[1:]
+                if not chain:
+                    chains.remove(chain)
 
-        for i, c in enumerate(todo):
-            for cb in SZ2[i]:
-                z_pass(cb, 1)
-            for cb in SA2[i]:
-                z_sums(cb, 1)
-            if i == G_S and SCB:
-                ops = ops + norm_ops(0, SCB)
-            now = wait[: FIN_AT[i]]
-            wait = wait[FIN_AT[i] :]
-            for f in now:
-                finish_s(*f)
-            for half in (stat1, stat2):
-                half(*c)
-                ops = norm_some(OPS)
-            conv_next(1 + len(SZ2[i]))
-            for f in now:
-                finish(*f)
-            if c[1] == BS - 1 and c[0] + 1 in GROUPS:
-                ops = ops + norm_ops(start, c[0] + 1)
-                start = c[0] + 1
-        head = wait[:DRAIN]
-        for f in head:
-            finish_s(*f)
-        ops = norm_some(len(ops))
-        for i, f in enumerate(wait):
-            if i >= len(head):
-                finish_s(*f)
-            finish(*f)
+        convs(2)
+        going = []
+        for i in range(len(blocks)):
+            if i % 2 == 0 and i // 2 < ZB:
+                z_products(i // 2, 1)
+            if i % 2 == 0 and 1 <= i // 2 <= ZB:
+                z_sums(i // 2 - 1, 1)
+            if i == 2 * ZB + 1:
+                chains.append(norm_steps(0, ZB))
+            cv_turns(ROUNDS + 1 + i)
+            if i == 5:
+                mask_banks.extend(mask_bank(b) for b in range(BS))
+            stat1(*blocks[i])
+            cv_quants(ROUNDS + 1 + i)
+            small_steps()
+            if i > 0:
+                stat2(*blocks[i - 1])
+                small_steps()
+            convs(2 if i % 2 == 0 and i // 2 < ZB else 1)
+            for block in going:
+                finish(*block)
+                small_steps()
+            going = ready[:2]
+            ready[:] = ready[2:]
+            for block in going:
+                scale(*block)
+            if i > 0 and blocks[i - 1] == (ZB, BS - 1):
+                chains.append(norm_steps(ZB, ZB + 1))
+            if i > 0 and blocks[i - 1] == (last - 1, BS - 1):
+                chains.append(norm_steps(ZB + 1, last))
+        chains.append(last_norm_steps())
+        stat2(*blocks[-1])
+        for i in range(2 * CB):
+            small_steps()
+            if going:
+                finish(*going[0])
+                going = going[1:]
+            if ready and len(going) < 3:
+                scale(*ready[0])
+                going = going + ready[:1]
+                ready[:] = ready[1:]

from contextlib import ExitStack

import concourse.mybir as mybir
from concourse.masks import make_identity

BS, NF, N, J, NOUT = 2, 512, 512, 3, 512
KC = J * NF
EPS = 1e-5
P = 128
T = 4
MB = N // P
CB = 2 * NOUT // P
ROUNDS = BS * (MB // 2) * J

F32 = mybir.dt.float32
BF16 = mybir.dt.bfloat16
U32 = mybir.dt.uint32
U8 = mybir.dt.uint8
FP8 = mybir.dt.float8_e4m3fn
FP8X4 = mybir.dt.float8_e4m3fn_x4
ALU = mybir.AluOpType
ACT = mybir.ActivationFunctionType

FLOPS = 2 * BS * J * N * N * NF + 2 * BS * 2 * NOUT * KC * N

BANKS = {"w": 2, "x1": 3, "turn": 2, "spare": 1}
Y_BANKS = ("x1", "w", "spare", "x1", "w", "x1")
CV_STEP = (0, 0, 1, 1, 5, 6, 7, 11, 11, 12, 12, 13)
CV_ON_VECTOR = (7, 8)
ZB = 3
Z_ROUND = 7


def tile_layer_simple_pa_kernel(
    tc, X, W_bytes, W_scale, N_batch, mask, cv1_w, cv1_b, cv2_w, cv2_b, bn_gamma, bn_beta, out
):
    nc = tc.nc
    v = nc.vector
    g = nc.gpsimd
    with ExitStack() as ctx:
        keep = ctx.enter_context(tc.tile_pool(name="keep", bufs=1))
        work = ctx.enter_context(tc.tile_pool(name="work", bufs=3))
        psum = ctx.enter_context(tc.psum_pool(name="psum", bufs=1))
        ctx.enter_context(tc.manual_schedule())

        def bank(shape, dtype, name):
            return psum.tile(shape, dtype, name=name, bufs=BANKS[name])

        w_scale = keep.tile([P, T], F32)
        nc.scalar.dma_start(out=w_scale[:], in_=W_scale[0, 0].rearrange("(p t) o -> p (t o)", t=T))

        w_codes = []
        x_rows = []
        cv_rows = []

        def load_w(i):
            b, mb = divmod(i, MB)
            codes = keep.tile([P, N * J], U8, name=f"w_codes{i}")
            nc.sync.dma_start(
                out=codes[:], in_=W_bytes[b].rearrange("(mb p) n j -> mb p (n j)", p=P)[mb]
            )
            w_codes.append(codes)

        def load_x(b):
            rows = keep.tile([P, T, N], BF16, name=f"x_rows{b}")
            for h in range(2):
                nc.sync.dma_start(
                    out=rows[:, 2 * h : 2 * h + 2, :],
                    in_=X[b].rearrange("(p t) n -> p t n", t=T)[:, 2 * h : 2 * h + 2, :],
                )
            x_rows.append(rows)

        def load_cv(cb):
            src = cv2_w if cb < CB // 2 else cv1_w
            rows = keep.tile([P, KC], BF16, name=f"cv_rows{cb}")
            r0 = (cb % (CB // 2)) * P
            nc.sync.dma_start(out=rows[:], in_=src[r0 : r0 + P, :])
            cv_rows.append(rows)

        ident_b = keep.tile([P, P], BF16)
        make_identity(nc, ident_b[:])
        ident_f = keep.tile([P, P], F32)
        make_identity(nc, ident_f[:])
        mask_row = keep.tile([P, BS * N], BF16)
        vec_rows = keep.tile([P, P], BF16)
        g.memset(vec_rows[:], 0.0)
        g.memset(mask_row[:], 0.0)
        ones = keep.tile([P, P], BF16)
        g.memset(ones[:], 1.0)

        load_w(0)
        load_w(1)
        load_w(2)
        load_x(0)
        load_w(3)
        load_cv(0)
        load_cv(1)
        for b in range(BS):
            nc.sync.dma_start(out=mask_row[0:1, b * N : (b + 1) * N], in_=mask[b])
        nc.sync.dma_start(out=vec_rows[0:4, :], in_=cv2_b.rearrange("(r c) -> r c", c=P))
        nc.sync.dma_start(out=vec_rows[4:8, :], in_=cv1_b.rearrange("(r c) -> r c", c=P))
        nc.sync.dma_start(out=vec_rows[8:16, :], in_=bn_gamma.rearrange("(r c) -> r c", c=P))
        nc.sync.dma_start(out=vec_rows[16:24, :], in_=bn_beta.rearrange("(r c) -> r c", c=P))
        counts = keep.tile([P, BS], BF16)
        nc.sync.dma_start(out=counts[:], in_=N_batch.partition_broadcast(P))
        load_w(4)
        load_cv(2)
        load_x(1)
        load_w(5)
        load_cv(3)
        load_w(6)
        load_w(7)
        for cb in range(4, CB):
            load_cv(cb)

        one = keep.tile([P, 1], F32)
        v.memset(one[:], 1.0)
        table = keep.tile([P, 1], F32)
        nc.scalar.activation(out=table[:], in_=one[:], func=ACT.Abs_reciprocal_sqrt)

        zeros = keep.tile([P, N], BF16)
        v.memset(zeros[:], 0.0)

        def idle_matmul():
            ps = bank([P, N], F32, "spare")
            nc.tensor.matmul(ps[:], lhsT=zeros[:, 0:P], rhs=zeros[:], start=True, stop=True)

        x_q = [keep.tile([P, T * P], U32, name=f"x_q{b}", align_bytes=64) for b in range(BS)]
        x_s = [keep.tile([P, T * P], U8, name=f"x_s{b}", align_bytes=64) for b in range(BS)]
        x_t = {}

        def x_turn(b):
            x_t[b] = work.tile([P, T * P * T], BF16, name="x_t", bufs=2, align_bytes=64)
            pairs = x_rows[b][:].bitcast(F32).rearrange("p t (q u) -> p t u q", u=2)
            for h in range(2):
                ps = bank([P, 2, 2, P], F32, "turn")
                for i in range(2):
                    for u in range(2):
                        nc.tensor.transpose(ps[:, i, u, :], pairs[:, 2 * h + i, u, :], ident_f[:])
                half = x_t[b][:, h * 1024 : (h + 1) * 1024].bitcast(F32)
                nc.scalar.copy(
                    out=half.rearrange("p (i f u) -> p i f u", i=2, u=2), in_=ps[:].rearrange("p i u f -> p i f u")
                )

        def x_quant(b):
            v.quantize_mx(out=x_q[b][:].bitcast(FP8X4), scales=x_s[b][:], in_=x_t[b][:])

        cv_q = keep.tile([P, CB * J, P], U32, align_bytes=64)
        cv_s = keep.tile([P, CB * J, P], U8, align_bytes=64)
        cv_t = {}

        def cv_turn(h):
            if h % 2 == 0:
                cv_t[h // 2] = work.tile([P, 4 * P * T], BF16, name="cv_t", bufs=2, align_bytes=64)
            ps = bank([P, 2, 2, P], F32, "turn")
            for i in range(2):
                cb, j = divmod(2 * h + i, J)
                pairs = cv_rows[cb][:].bitcast(F32).rearrange("p (j q u) -> p j u q", j=J, u=2)
                for u in range(2):
                    nc.tensor.transpose(ps[:, i, u, :], pairs[:, j, u, :], ident_f[:])
            o = (h % 2) * 1024
            dst = cv_t[h // 2][:, o : o + 1024].bitcast(F32).rearrange("p (i c u) -> p i c u", i=2, u=2)
            src = ps[:].rearrange("p i u c -> p i c u")
            if h in CV_ON_VECTOR:
                v.tensor_copy(out=dst, in_=src)
            else:
                nc.scalar.copy(out=dst, in_=src)

        def cv_turns(step):
            for h in range(len(CV_STEP)):
                if CV_STEP[h] == step:
                    cv_turn(h)

        def cv_quants(step):
            for h in range(1, len(CV_STEP), 2):
                if CV_STEP[h] == step - 1:
                    four = slice(2 * h - 2, 2 * h + 2)
                    v.quantize_mx(
                        out=cv_q[:, four, :].rearrange("p g c -> p (g c)").bitcast(FP8X4),
                        scales=cv_s[:, four, :].rearrange("p g c -> p (g c)"),
                        in_=cv_t[h // 2][:],
                    )

        x1_t = [keep.tile([P, J, N * T], BF16, name=f"x1_t{b}", align_bytes=64) for b in range(BS)]
        x1_q = [keep.tile([P, J, N], U32, name=f"x1_q{b}", align_bytes=64) for b in range(BS)]
        x1_s = [keep.tile([P, J, N], U8, name=f"x1_s{b}", align_bytes=64) for b in range(BS)]
        scale_words = w_scale[:].rearrange("p (u e) -> p u e", u=2).unsqueeze(1).to_broadcast([P, 2 * P, 2, 2])
        w_wide = {}
        w_banks = {}
        w_t = {}
        w_q = {}
        x1_banks = {}

        def widen(i):
            w_wide[i] = work.tile([P, J, N], BF16, name="w_wide", bufs=6)
            v.tensor_scalar(
                out=w_wide[i][:].rearrange("p j n -> p n j"),
                in0=w_codes[i][:].rearrange("p (n j) -> p n j", j=J).bitcast(FP8),
                scalar1=one[:],
                scalar2=None,
                op0=ALU.mult,
            )

        def w_turn(r):
            s, j = divmod(r, J)
            w_banks[r] = bank([P, 2, 2 * P], F32, "w")
            for h in range(2):
                pairs = w_wide[2 * s + h][:, j, :].bitcast(F32).rearrange("p (q u) -> p u q", u=2)
                for u in range(2):
                    nc.tensor.transpose(w_banks[r][:, u, h * P : (h + 1) * P], pairs[:, u, :], ident_f[:])

        def w_product(r):
            w_t[r] = work.tile([P, 2 * P * T], BF16, name="w_t", align_bytes=64)
            values = w_banks[r][:].rearrange("p u m -> p (u m)").bitcast(BF16)
            v.tensor_tensor(
                out=w_t[r][:].rearrange("p (m u e) -> p m u e", u=2, e=2),
                in0=values.rearrange("p (u m e) -> p m u e", u=2, e=2),
                in1=scale_words,
                op=ALU.mult,
            )

        def w_quant(r):
            q = work.tile([P, 2 * P], U32, name="w_q", align_bytes=64)
            s = work.tile([P, 2 * P], U8, name="w_s", align_bytes=64)
            v.quantize_mx(out=q[:].bitcast(FP8X4), scales=s[:], in_=w_t[r][:])
            w_q[r] = (q, s)

        def step1(r, h):
            b = r // (2 * J)
            q, s = w_q[r]
            nodes = slice(h * P, (h + 1) * P)
            x1_banks[r, h] = bank([P, T, P], F32, "x1")
            for t in range(T):
                nc.tensor.matmul_mx(
                    out=x1_banks[r, h][:, t, :],
                    lhsT=x_q[b][:, t * P : (t + 1) * P].bitcast(FP8X4),
                    lhsT_scale=x_s[b][:, t * P : (t + 1) * P],
                    rhs=q[:, nodes].bitcast(FP8X4),
                    rhs_scale=s[:, nodes],
                    start=True,
                    stop=True,
                )

        def x1_copy(r, h):
            s, j = divmod(r, J)
            c0 = (2 * (s % 2) + h) * P * T
            nc.scalar.copy(
                out=x1_t[s // 2][:, j, c0 : c0 + P * T].rearrange("p (m t) -> p m t", t=T),
                in_=x1_banks[r, h][:].rearrange("p t m -> p m t"),
            )

        def x1_quant(r):
            s, j = divmod(r, J)
            b = s // 2
            c0 = (s % 2) * 2 * P
            v.quantize_mx(
                out=x1_q[b][:, j, c0 : c0 + 2 * P].bitcast(FP8X4),
                scales=x1_s[b][:, j, c0 : c0 + 2 * P],
                in_=x1_t[b][:, j, c0 * T : (c0 + 2 * P) * T],
            )

        vec = keep.tile([P, 3 * CB], F32)
        bias = vec[:, 0:CB]
        gamma = vec[:, CB : 2 * CB]
        beta = vec[:, 2 * CB : 3 * CB]
        mk = keep.tile([P, BS, N], F32)
        mask_sums = keep.tile([P, BS], F32)
        eps = keep.tile([P, 1], F32)
        neg_bias = keep.tile([P, CB], F32)
        total = keep.tile([P, 1], F32)
        rtotal = keep.tile([P, 1], F32)
        mask_sum = keep.tile([P, 1], F32)
        ratio1 = keep.tile([P, 1], F32)
        shift = keep.tile([P, CB], F32)
        c1 = keep.tile([P, 1], F32)
        c1r = keep.tile([P, 1], F32)
        c2 = keep.tile([P, CB], F32)
        c3 = keep.tile([P, CB], F32)

        def mask_bank(b):
            ps = bank([P, N], F32, "turn")
            nc.tensor.matmul(
                ps[:], lhsT=ones[:], rhs=mask_row[:, b * N : (b + 1) * N], start=True, stop=True
            )
            return ps

        def vectors():
            ps = bank([P, P], BF16, "turn")
            nc.tensor.transpose(ps[:], vec_rows[:], ident_b[:])
            v.tensor_copy(out=vec[:], in_=ps[:, 0 : 3 * CB])
            for b in range(BS):
                nc.scalar.activation(
                    out=mk[:, b, :], in_=mask_bank(b)[:], func=ACT.Copy, accum_out=mask_sums[:, b : b + 1]
                )
            g.tensor_tensor(out=total[:], in0=counts[:, 0:1], in1=counts[:, 1:2], op=ALU.add)
            g.tensor_scalar(out=eps[:], in0=total[:], scalar1=0.0, scalar2=EPS, op0=ALU.mult, op1=ALU.add)
            g.tensor_scalar(out=neg_bias[:], in0=bias, scalar1=-1.0, scalar2=0.0, op0=ALU.mult, op1=ALU.add)
            v.reciprocal(out=rtotal[:], in_=total[:])
            g.tensor_tensor(out=mask_sum[:], in0=mask_sums[:, 0:1], in1=mask_sums[:, 1:2], op=ALU.add)
            g.tensor_scalar(
                out=ratio1[:], in0=mask_sum[:], scalar1=rtotal[:], scalar2=1.0, op0=ALU.mult, op1=ALU.subtract
            )
            g.memset(shift[:, 0:ZB], 0.0)
            g.tensor_scalar(
                out=shift[:, ZB:], in0=bias[:, ZB:], scalar1=ratio1[:], scalar2=0.0, op0=ALU.mult, op1=ALU.add
            )
            g.tensor_scalar(
                out=c1[:], in0=total[:], scalar1=-2.0, scalar2=mask_sum[:], op0=ALU.mult, op1=ALU.add
            )
            g.tensor_scalar(out=c2[:], in0=shift[:], scalar1=total[:], scalar2=2.0, op0=ALU.mult, op1=ALU.mult)
            g.tensor_tensor(out=c1r[:], in0=rtotal[:], in1=c1[:], op=ALU.mult)
            g.tensor_scalar(out=c3[:], in0=shift[:], scalar1=c1[:], scalar2=0.0, op0=ALU.mult, op1=ALU.add)
            g.tensor_tensor(out=c3[:], in0=c3[:], in1=c2[:], op=ALU.add)

        sums = keep.tile([P, 2, BS, CB], F32)
        y_banks = {}
        kept = {}
        squares = {}

        def conv(cb, b, name):
            y_banks[cb, b] = bank([P, N], F32, name)
            for j in range(J):
                nc.tensor.matmul_mx(
                    out=y_banks[cb, b][:],
                    lhsT=cv_q[:, cb * J + j, :].bitcast(FP8X4),
                    lhsT_scale=cv_s[:, cb * J + j, :],
                    rhs=x1_q[b][:, j, :].bitcast(FP8X4),
                    rhs_scale=x1_s[b][:, j, :],
                    start=(j == 0),
                    stop=(j == J - 1),
                )

        def stat1(cb, b):
            kept[cb, b] = work.tile([P, N], F32, name="kept", bufs=2 * CB)
            v.scalar_tensor_tensor(
                out=kept[cb, b][:], in0=y_banks[cb, b][:], scalar=neg_bias[:, cb : cb + 1], in1=mk[:, b, :],
                op0=ALU.max, op1=ALU.mult, accum_out=sums[:, 0, b, cb : cb + 1],
            )

        def stat2(cb, b):
            unread = work.tile([P, N], F32, name="unread_v", bufs=2)
            v.scalar_tensor_tensor(
                out=unread[:], in0=y_banks[cb, b][:], scalar=neg_bias[:, cb : cb + 1], in1=kept[cb, b][:],
                op0=ALU.max, op1=ALU.mult, accum_out=sums[:, 1, b, cb : cb + 1],
            )

        def z_products(cb, b):
            z = work.tile([P, N], F32, name="kept", bufs=2 * CB)
            nc.scalar.activation(out=z[:], in_=y_banks[cb, b][:], func=ACT.Relu, bias=bias[:, cb : cb + 1])
            zm = work.tile([P, N], F32, name="zm", bufs=3)
            g.tensor_tensor(out=zm[:], in0=z[:], in1=mk[:, b, :], op=ALU.mult)
            zzm = work.tile([P, N], F32, name="zzm", bufs=3)
            g.tensor_tensor(out=zzm[:], in0=z[:], in1=zm[:], op=ALU.mult)
            kept[cb, b] = z
            squares[cb, b] = (zm, zzm)

        def z_sums(cb, b):
            for i, product in enumerate(squares[cb, b]):
                unread = work.tile([P, N], F32, name="unread_s", bufs=2)
                nc.scalar.activation(
                    out=unread[:], in_=product[:], func=ACT.Copy, accum_out=sums[:, i, b, cb : cb + 1]
                )

        both = keep.tile([P, 2, CB], F32)
        d = keep.tile([P, CB], F32)
        c1d_c2 = keep.tile([P, CB], F32)
        var_part = keep.tile([P, CB], F32)
        var_sum = keep.tile([P, CB], F32)
        neg_gd = keep.tile([P, CB], F32)
        rstd = keep.tile([P, CB], F32)
        neg_fd = keep.tile([P, CB], F32)
        factor = keep.tile([P, CB], F32)
        offset = keep.tile([P, CB], F32)

        def norm_steps(lo, hi):
            c = slice(lo, hi)

            def add_graphs():
                v.tensor_tensor(out=both[:, :, c], in0=sums[:, :, 0, c], in1=sums[:, :, 1, c], op=ALU.add)

            def means():
                v.scalar_tensor_tensor(
                    out=d[:, c], in0=both[:, 0, c], scalar=rtotal[:], in1=shift[:, c], op0=ALU.mult, op1=ALU.add
                )
                v.scalar_tensor_tensor(
                    out=c1d_c2[:, c], in0=both[:, 0, c], scalar=c1r[:], in1=c3[:, c], op0=ALU.mult, op1=ALU.add
                )

            def products():
                v.tensor_tensor(out=var_part[:, c], in0=d[:, c], in1=c1d_c2[:, c], op=ALU.mult)
                v.scalar_tensor_tensor(
                    out=neg_gd[:, c], in0=d[:, c], scalar=-1.0, in1=gamma[:, c], op0=ALU.mult, op1=ALU.mult
                )

            def roots():
                v.tensor_tensor(out=var_sum[:, c], in0=var_part[:, c], in1=both[:, 1, c], op=ALU.add)
                nc.scalar.activation(
                    out=rstd[:, c], in_=var_sum[:, c], func=ACT.Abs_reciprocal_sqrt, scale=rtotal[:], bias=eps[:]
                )

            def factors():
                v.tensor_tensor(out=neg_fd[:, c], in0=rstd[:, c], in1=neg_gd[:, c], op=ALU.mult)
                v.tensor_tensor(out=factor[:, c], in0=rstd[:, c], in1=gamma[:, c], op=ALU.mult)

            def offsets():
                v.tensor_tensor(out=offset[:, c], in0=neg_fd[:, c], in1=beta[:, c], op=ALU.add)
                ready.extend((cb, b) for cb in range(lo, hi) for b in range(BS))

            return [add_graphs, means, products, roots, None, factors, offsets]

        last = CB - 1
        l_sum, l_d, l_c1d_c2, l_var, l_var_eps, l_neg_gd, l_rstd = (
            keep.tile([P, 1], F32, name=f"last{i}") for i in range(7)
        )

        def last_norm_steps():
            c = slice(last, CB)

            def add_graphs():
                v.tensor_tensor(out=l_sum[:], in0=sums[:, 0, 0, c], in1=sums[:, 0, 1, c], op=ALU.add)

            def means():
                v.tensor_scalar(
                    out=l_d[:], in0=l_sum[:], scalar1=rtotal[:], scalar2=shift[:, c], op0=ALU.mult, op1=ALU.add
                )
                v.tensor_scalar(
                    out=l_c1d_c2[:], in0=l_sum[:], scalar1=c1r[:], scalar2=c3[:, c], op0=ALU.mult, op1=ALU.add
                )

            def products():
                v.scalar_tensor_tensor(
                    out=l_var[:], in0=l_d[:], scalar=l_c1d_c2[:], in1=sums[:, 1, 0, c], op0=ALU.mult, op1=ALU.add
                )
                v.scalar_tensor_tensor(
                    out=l_neg_gd[:], in0=l_d[:], scalar=-1.0, in1=gamma[:, c], op0=ALU.mult, op1=ALU.mult
                )

            def add_eps():
                v.tensor_scalar(
                    out=l_var_eps[:], in0=l_var[:], scalar1=rtotal[:], scalar2=EPS, op0=ALU.mult, op1=ALU.add
                )

            def root():
                nc.scalar.activation(
                    out=l_rstd[:], in_=sums[:, 1, 1, c], func=ACT.Abs_reciprocal_sqrt, scale=rtotal[:], bias=l_var_eps[:]
                )

            def factors():
                v.scalar_tensor_tensor(
                    out=offset[:, c], in0=l_rstd[:], scalar=l_neg_gd[:], in1=beta[:, c], op0=ALU.mult, op1=ALU.add
                )
                v.tensor_tensor(out=factor[:, c], in0=l_rstd[:], in1=gamma[:, c], op=ALU.mult)
                ready.extend((last, b) for b in range(BS))

            return [add_graphs, means, products, add_eps, root, None, factors]

        mask_banks = []
        scaled = {}

        def scale(cb, b):
            scaled[cb, b] = work.tile([P, N], F32, name="scaled", bufs=5)
            f = factor[:, cb : cb + 1]
            if cb < ZB:
                nc.scalar.activation(
                    out=scaled[cb, b][:], in_=kept[cb, b][:], func=ACT.Identity, scale=f, bias=offset[:, cb : cb + 1]
                )
            else:
                nc.scalar.activation(out=scaled[cb, b][:], in_=kept[cb, b][:], func=ACT.Copy, scale=f)

        def finish(cb, b):
            o = work.tile([P, N], F32, name="o", bufs=7)
            if cb < ZB:
                v.tensor_tensor(out=o[:], in0=mask_banks[b][:], in1=scaled[cb, b][:], op=ALU.mult)
            else:
                v.scalar_tensor_tensor(
                    out=o[:], in0=mask_banks[b][:], scalar=offset[:, cb : cb + 1], in1=scaled[cb, b][:],
                    op0=ALU.mult, op1=ALU.add,
                )
            nc.sync.dma_start(out=out[b, cb * P : (cb + 1) * P, :], in_=o[:])

        for i in range(3):
            widen(i)
        w_turn(0)
        x_turn(0)
        for r in range(ROUNDS + 1):
            if r == 1:
                x_quant(0)
            if r + 1 < ROUNDS:
                w_turn(r + 1)
            if r > 0:
                w_quant(r - 1)
                for h in range(2):
                    step1(r - 1, h)
                    x1_copy(r - 1, h)
            if r in (3, 5, 7, 9):
                idle_matmul()
            if r < ROUNDS:
                w_product(r)
            if r in (0, 1, 3, 5, 7):
                widen(3 + (r + 1) // 2)
            if r == 3:
                x_turn(1)
            if r == 4:
                x_quant(1)
                vectors()
            cv_turns(r)
            if r >= 2:
                x1_quant(r - 2)
            cv_quants(r)
            cb, odd = divmod(r - Z_ROUND, 2)
            if odd == 0 and 1 <= cb <= ZB:
                z_sums(cb - 1, 0)
            if odd == 0 and 0 <= cb < ZB:
                conv(cb, 0, "spare")
                z_products(cb, 0)
        x1_quant(ROUNDS - 1)
        z_sums(ZB - 1, 0)

        blocks = [(cb, b) for cb in range(ZB, CB) for b in range(BS)]
        order = []
        for i in range(len(blocks)):
            if i % 2 == 0 and i // 2 < ZB:
                order.append((i // 2, 1))
            order.append(blocks[i])
        issued = []

        def convs(n):
            for cb, b in order[len(issued) : len(issued) + n]:
                conv(cb, b, Y_BANKS[len(issued) % len(Y_BANKS)])
                issued.append((cb, b))

        chains = []
        ready = []

        def small_steps():
            for chain in list(chains):
                if chain[0] is not None:
                    chain[0]()
                chain[:] = chain[1:]
                if not chain:
                    chains.remove(chain)

        convs(2)
        going = []
        for i in range(len(blocks)):
            if i % 2 == 0 and i // 2 < ZB:
                z_products(i // 2, 1)
            if i % 2 == 0 and 1 <= i // 2 <= ZB:
                z_sums(i // 2 - 1, 1)
            if i == 2 * ZB + 1:
                chains.append(norm_steps(0, ZB))
            cv_turns(ROUNDS + 1 + i)
            if i == 5:
                mask_banks.extend(mask_bank(b) for b in range(BS))
            stat1(*blocks[i])
            cv_quants(ROUNDS + 1 + i)
            small_steps()
            if i > 0:
                stat2(*blocks[i - 1])
                small_steps()
            convs(2 if i % 2 == 0 and i // 2 < ZB else 1)
            for block in going:
                finish(*block)
                small_steps()
            going = ready[:2]
            ready[:] = ready[2:]
            for block in going:
                scale(*block)
            if i > 0 and blocks[i - 1] == (ZB, BS - 1):
                chains.append(norm_steps(ZB, ZB + 1))
            if i > 0 and blocks[i - 1] == (last - 1, BS - 1):
                chains.append(norm_steps(ZB + 1, last))
        chains.append(last_norm_steps())
        stat2(*blocks[-1])
        for i in range(2 * CB):
            small_steps()
            if going:
                finish(*going[0])
                going = going[1:]
            if ready and len(going) < 3:
                scale(*ready[0])
                going = going + ready[:1]
                ready[:] = ready[1:]
